import numpy as np
import ml_dtypes


def mxq(x, axis, fmt="e4m3"):
    dtype, down = {"e4m3": (ml_dtypes.float8_e4m3fn, 7), "e5m2": (ml_dtypes.float8_e5m2, 14)}[fmt]
    v = np.moveaxis(np.asarray(x, np.float32).astype(ml_dtypes.bfloat16).astype(np.float64), axis, -1)
    blocks = v.reshape(v.shape[:-1] + (-1, 32))
    amax = np.abs(blocks).max(-1, keepdims=True)
    byte = np.maximum(np.where(amax > 0, np.frexp(amax)[1] - 1 + 127, 0) - down, 1)
    scale = np.exp2(byte - 127.0)
    codes = (blocks / scale).astype(np.float32).astype(dtype).astype(np.float64)
    return np.moveaxis((codes * scale).reshape(v.shape), -1, axis)


WIDE = False


def mx_kscale(k):
    if not WIDE:
        return np.ones(k)
    levels = np.array([10, -10, 5, -5, 0])
    a = np.random.permutation(np.resize(levels, k // 512 * 4)).reshape(k // 512, 4)
    idx = np.arange(k)
    return np.exp2(a[idx // 512, idx % 128 // 32])


BF16 = ml_dtypes.bfloat16


def bf(x):
    return np.asarray(x, np.float32).astype(BF16)


def f64(x):
    return np.asarray(x).astype(np.float64)


N, N_CH, X, H = 512, 5, 512, 512
K = N_CH * H


def sigmoid(v):
    return 1.0 / (1.0 + np.exp(-v))


def setup_inputs():
    s, t = mx_kscale(X), mx_kscale(K)
    return {
        "x": bf(np.random.standard_normal((N, X)) * s),
        "x_mask": bf(np.random.random(N) < 0.75),
        "neighbour_h": bf(np.random.standard_normal((N, N_CH, H)) * t.reshape(N_CH, H)),
        "neighbour_c": bf(np.random.standard_normal((N, N_CH, H))),
        "W_f_in": bf(np.random.standard_normal((X, H)) * 0.5 / np.sqrt(X) / s[:, None]),
        "b_f_in": bf(np.random.standard_normal(H) * 0.3),
        "W_aggr_f": bf(np.random.standard_normal((K, K)) / np.sqrt(K) / t[:, None]),
        "b_aggr_f": bf(np.random.standard_normal(K) * 0.3),
    }


def reference(x, x_mask, neighbour_h, neighbour_c, W_f_in, b_f_in, W_aggr_f, b_aggr_f):
    h_flat = f64(neighbour_h).reshape(N, K)
    f_input = ((mxq(f64(x), 1, "e4m3") @ mxq(f64(W_f_in), 0, "e4m3")) + f64(b_f_in)) * f64(x_mask)[:, None]
    f_input = np.tile(f_input, (1, N_CH))
    f_gate = (mxq(h_flat, 1, "e4m3") @ mxq(f64(W_aggr_f), 0, "e4m3")) + f64(b_aggr_f) + f_input
    f_aggr = f_gate + f_input
    f = sigmoid(f_aggr).reshape(N, N_CH, H)
    return np.sum(f * f64(neighbour_c), axis=1)

@@ -1,0 +1,317 @@
+import concourse.mybir as mybir
+from concourse.masks import make_identity
+
+F32 = mybir.dt.float32
+BF16 = mybir.dt.bfloat16
+U32 = mybir.dt.uint32
+U8 = mybir.dt.uint8
+FP8X4 = mybir.dt.float8_e4m3fn_x4
+ADD = mybir.AluOpType.add
+MULT = mybir.AluOpType.mult
+SIGMOID = mybir.ActivationFunctionType.Sigmoid
+
+P = 128
+PACK = 4
+K_PASS = P * PACK
+NODES = 512
+CHILDREN = 5
+FEATURES = 512
+NODE_TILES = NODES // P
+FEATURE_TILES = FEATURES // P
+H_PASSES = CHILDREN * FEATURES // K_PASS
+CHUNKS = CHILDREN * H_PASSES
+HALF = NODES // 2
+
+RAW_BUFS = 10
+VECTOR_COLS = 192
+RUN = 4
+
+FLOPS = 2 * NODES * (CHILDREN * FEATURES) ** 2 + 2 * NODES * FEATURES * FEATURES
+
+
+def tile_treelstmcell_pa_kernel(
+    tc, x, x_mask, neighbour_h, neighbour_c, W_f_in, b_f_in, W_aggr_f, b_aggr_f, out
+):
+    nc = tc.nc
+    hf = neighbour_h.rearrange("n c f -> n (c f)")
+
+    with tc.tile_pool(name="const", bufs=1) as const, tc.tile_pool(
+        name="raw", bufs=RAW_BUFS
+    ) as raw_pool, tc.tile_pool(name="stage", bufs=3) as stage, tc.tile_pool(
+        name="codes", bufs=2
+    ) as codes_pool, tc.tile_pool(name="work", bufs=3) as work, tc.psum_pool(
+        name="sums", bufs=1
+    ) as psum_sums, tc.psum_pool(name="acc", bufs=2) as psum_acc, tc.psum_pool(
+        name="flip", bufs=2
+    ) as psum_flip:
+        h_sb = []
+        for nt in range(NODE_TILES):
+            h_tile = const.tile([P, CHILDREN * FEATURES], BF16, name="h_sb%d" % nt)
+            nc.sync.dma_start(out=h_tile[:], in_=hf[nt * P : (nt + 1) * P, :])
+            h_sb.append(h_tile)
+        x_sb = const.tile([P, NODE_TILES * FEATURES], BF16)
+        nc.sync.dma_start(
+            out=x_sb[:].rearrange("p (t k) -> p t k", t=NODE_TILES),
+            in_=x.rearrange("(t p) k -> p t k", p=P),
+        )
+        wf_raw = const.tile([P, PACK, FEATURES], BF16)
+        nc.sync.dma_start(out=wf_raw[:], in_=W_f_in.rearrange("(p t) n -> p t n", t=PACK))
+
+        raw_of = {}
+        c_sb = {}
+
+        def load_chunk(chunk):
+            child, g = divmod(chunk, H_PASSES)
+            raw = raw_pool.tile([P, PACK, FEATURES], BF16, tag="raw")
+            nc.sync.dma_start(
+                out=raw[:],
+                in_=W_aggr_f[
+                    g * K_PASS : (g + 1) * K_PASS, child * FEATURES : (child + 1) * FEATURES
+                ].rearrange("(p t) n -> p t n", t=PACK),
+            )
+            raw_of[chunk] = raw
+            if g == H_PASSES - 1:
+                cells = const.tile([P, NODE_TILES, FEATURES], BF16, name="c_sb%d" % child)
+                nc.sync.dma_start(
+                    out=cells[:], in_=neighbour_c[:, child, :].rearrange("(t p) f -> p t f", p=P)
+                )
+                c_sb[child] = cells
+
+        for chunk in range(RAW_BUFS):
+            load_chunk(chunk)
+
+        bias_rows = const.tile([P, P], BF16)
+        nc.vector.memset(bias_rows[:], 0.0)
+        aggr_rows = CHILDREN * FEATURE_TILES
+        nc.scalar.dma_start(
+            out=bias_rows[0:aggr_rows, :], in_=b_aggr_f.rearrange("(r m) -> r m", m=P)
+        )
+        nc.scalar.dma_start(
+            out=bias_rows[aggr_rows : aggr_rows + FEATURE_TILES, :],
+            in_=b_f_in.rearrange("(r m) -> r m", m=P),
+        )
+        mask_rows = const.tile([P, NODES], BF16)
+        nc.vector.memset(mask_rows[:], 0.0)
+        nc.scalar.dma_start(out=mask_rows[0:1, :], in_=x_mask.rearrange("(o n) -> o n", o=1))
+
+        ident_f32 = const.tile([P, P], F32)
+        make_identity(nc, ident_f32[:])
+        ident_bf = const.tile([P, P], BF16)
+        make_identity(nc, ident_bf[:])
+        twos = const.tile([P, P], BF16)
+        nc.vector.memset(twos[:], 2.0)
+
+        warm = const.tile([P, 2], F32)
+        nc.vector.memset(warm[:], 0.0)
+        nc.scalar.activation(out=warm[:, 1:2], in_=warm[:, 0:1], func=SIGMOID)
+
+        bias_ps = psum_flip.tile([P, P], BF16, tag="flip")
+        nc.tensor.transpose(bias_ps[:], bias_rows[:], ident_bf[:])
+        bias_cols = const.tile([P, P], F32)
+        nc.vector.tensor_copy(out=bias_cols[:], in_=bias_ps[:])
+
+        mask_ps = psum_acc.tile([P, NODES], F32, tag="acc")
+        nc.tensor.matmul(out=mask_ps[:], lhsT=twos[:], rhs=mask_rows[:], start=True, stop=True)
+        double_mask = const.tile([P, NODES], F32)
+        nc.vector.tensor_copy(out=double_mask[:], in_=mask_ps[:])
+
+        h_codes = const.tile([P, H_PASSES, NODES], U32, align_bytes=64)
+        h_scales = const.tile([P, H_PASSES, NODES], U8, align_bytes=64)
+        x_codes = const.tile([P, NODES], U32, align_bytes=64)
+        x_scales = const.tile([P, NODES], U8, align_bytes=64)
+
+        def flip_half(words_of, half):
+            bank = psum_flip.tile([P, 2, HALF], F32, tag="flip")
+            for side in range(2):
+                pairs = words_of(2 * half + side).rearrange("n (p u) -> n u p", u=2)
+                for u in range(2):
+                    nc.tensor.transpose(
+                        bank[:, u, side * P : (side + 1) * P], pairs[:, u, :], ident_f32[:]
+                    )
+            grouped = stage.tile([P, HALF * PACK], BF16, tag="flipped", align_bytes=64)
+            nc.scalar.copy(
+                out=grouped[:].bitcast(F32).rearrange("p (n u) -> p n u", u=2),
+                in_=bank[:].rearrange("p u n -> p n u"),
+            )
+            return grouped
+
+        def quantise(grouped, codes, scales):
+            nc.vector.quantize_mx(out=codes.bitcast(FP8X4), scales=scales, in_=grouped)
+
+        def h_words(g):
+            return lambda nt: h_sb[nt][:].bitcast(F32)[:, g * K_PASS // 2 : (g + 1) * K_PASS // 2]
+
+        def x_words(nt):
+            return x_sb[:].bitcast(F32)[:, nt * K_PASS // 2 : (nt + 1) * K_PASS // 2]
+
+        flips = []
+        for half in range(2):
+            for g in range(H_PASSES):
+                flips.append((h_words(g), half, h_codes[:, g, :], h_scales[:, g, :]))
+        for half in range(2):
+            flips.append((x_words, half, x_codes[:], x_scales[:]))
+
+        waiting = None
+        for words_of, half, codes, scales in flips:
+            grouped = flip_half(words_of, half)
+            if waiting is not None:
+                quantise(*waiting)
+            nodes = slice(half * HALF, (half + 1) * HALF)
+            waiting = (grouped[:], codes[:, nodes], scales[:, nodes])
+        quantise(*waiting)
+
+        def regroup(raw):
+            grouped = stage.tile([P, FEATURES, PACK], BF16, tag="grouped", align_bytes=64)
+            src = raw[:].rearrange("p t (c i) -> p c t i", i=RUN)
+            dst = grouped[:].rearrange("p (c i) t -> p c t i", i=RUN)
+            split = VECTOR_COLS // RUN
+            nc.vector.tensor_copy(out=dst[:, :split], in_=src[:, :split])
+            nc.scalar.copy(out=dst[:, split:], in_=src[:, split:])
+            return grouped
+
+        wf_codes = const.tile([P, FEATURES], U32, align_bytes=64)
+        wf_scales = const.tile([P, FEATURES], U8, align_bytes=64)
+        wf_grouped = regroup(wf_raw)
+        quantise(wf_grouped[:].rearrange("p c t -> p (c t)"), wf_codes[:], wf_scales[:])
+
+        input_term = []
+        for ft in range(FEATURE_TILES):
+            cols = slice(ft * P, (ft + 1) * P)
+            fi_ps = psum_acc.tile([P, NODES], F32, tag="acc")
+            nc.tensor.matmul_mx(
+                out=fi_ps[:],
+                lhsT=wf_codes[:, cols].bitcast(FP8X4),
+                lhsT_scale=wf_scales[:, cols],
+                rhs=x_codes[:].bitcast(FP8X4),
+                rhs_scale=x_scales[:],
+                start=True,
+                stop=True,
+            )
+            term = const.tile([P, NODES], F32, name="input_term%d" % ft)
+            nc.vector.scalar_tensor_tensor(
+                out=term[:],
+                in0=fi_ps[:],
+                scalar=bias_cols[:, aggr_rows + ft : aggr_rows + ft + 1],
+                in1=double_mask[:],
+                op0=ADD,
+                op1=MULT,
+            )
+            input_term.append(term)
+
+        out_sums = [
+            psum_sums.tile([P, FEATURES], F32, name="out_sums%d" % nt) for nt in range(NODE_TILES)
+        ]
+        grouped_of = {}
+        w_codes = {}
+        w_scales = {}
+        acc_of = {}
+        gate_of = {}
+        cells_t = {}
+
+        def quantise_chunk(chunk):
+            child, g = divmod(chunk, H_PASSES)
+            if g == 0:
+                w_codes[child] = codes_pool.tile(
+                    [P, H_PASSES, FEATURES], U32, tag="w_codes", name="w_codes", align_bytes=64
+                )
+                w_scales[child] = codes_pool.tile(
+                    [P, H_PASSES, FEATURES], U8, tag="w_scales", name="w_scales", align_bytes=64
+                )
+            quantise(
+                grouped_of[chunk][:].rearrange("p c t -> p (c t)"),
+                w_codes[child][:, g, :],
+                w_scales[child][:, g, :],
+            )
+
+        def multiply(child, ft):
+            cols = slice(ft * P, (ft + 1) * P)
+            acc = psum_acc.tile([P, NODES], F32, tag="acc")
+            for g in range(H_PASSES):
+                nc.tensor.matmul_mx(
+                    out=acc[:],
+                    lhsT=w_codes[child][:, g, cols].bitcast(FP8X4),
+                    lhsT_scale=w_scales[child][:, g, cols],
+                    rhs=h_codes[:, g, :].bitcast(FP8X4),
+                    rhs_scale=h_scales[:, g, :],
+                    start=(g == 0),
+                    stop=(g == H_PASSES - 1),
+                )
+            acc_of[(child, ft)] = acc
+
+        def squash(child, ft):
+            pre = work.tile([P, NODES], F32, tag="pre")
+            nc.vector.tensor_tensor(
+                out=pre[:], in0=acc_of[(child, ft)][:], in1=input_term[ft][:], op=ADD
+            )
+            gate = work.tile([P, NODES], F32, tag="gate")
+            tile_index = child * FEATURE_TILES + ft
+            nc.scalar.activation(
+                out=gate[:],
+                in_=pre[:],
+                func=SIGMOID,
+                bias=bias_cols[:, tile_index : tile_index + 1],
+                scale=1.0,
+            )
+            gate_of[(child, ft)] = gate
+
+        def flip_cells(child, pair):
+            bank = psum_flip.tile([P, 2, NODES], BF16, tag="flip")
+            for side in range(2):
+                ft = 2 * pair + side
+                for nt in range(NODE_TILES):
+                    nc.tensor.transpose(
+                        bank[:, side, nt * P : (nt + 1) * P],
+                        c_sb[child][:, nt, ft * P : (ft + 1) * P],
+                        ident_bf[:],
+                    )
+            cells_t[(child, pair)] = bank
+
+        def weigh_and_sum(child, ft):
+            weighted = work.tile([P, NODES], F32, tag="weighted")
+            nc.vector.tensor_tensor(
+                out=weighted[:],
+                in0=gate_of[(child, ft)][:],
+                in1=cells_t[(child, ft // 2)][:, ft % 2, :],
+                op=MULT,
+            )
+            for nt in range(NODE_TILES):
+                nc.tensor.matmul(
+                    out=out_sums[nt][:, ft * P : (ft + 1) * P],
+                    lhsT=weighted[:, nt * P : (nt + 1) * P],
+                    rhs=ident_f32[:],
+                    is_transpose=True,
+                    start=(child == 0 and ft == 0),
+                    stop=(child == CHILDREN - 1 and ft == FEATURE_TILES - 1),
+                )
+
+        def tile_at(slot, lag):
+            child, ft = divmod(slot - H_PASSES - lag, H_PASSES)
+            if 0 <= child < CHILDREN and ft < FEATURE_TILES:
+                return child, ft
+            return None
+
+        STAGES = 3
+        for slot in range(CHUNKS + FEATURE_TILES + STAGES - 1):
+            if slot < CHUNKS:
+                grouped_of[slot] = regroup(raw_of[slot])
+            if slot + RAW_BUFS < CHUNKS:
+                load_chunk(slot + RAW_BUFS)
+            if 1 <= slot <= CHUNKS:
+                quantise_chunk(slot - 1)
+            entering = tile_at(slot, 0)
+            if entering is not None:
+                multiply(*entering)
+            if tile_at(slot, 1) is not None:
+                squash(*tile_at(slot, 1))
+            if tile_at(slot, 2) is not None:
+                weigh_and_sum(*tile_at(slot, 2))
+            if entering is not None and entering[1] % 2 == 0:
+                flip_cells(entering[0], entering[1] // 2)
+
+        for nt in range(NODE_TILES):
+            result = work.tile([P, FEATURES], F32, tag="result")
+            if nt % 2 == 0:
+                nc.vector.tensor_copy(out=result[:], in_=out_sums[nt][:])
+            else:
+                nc.scalar.copy(out=result[:], in_=out_sums[nt][:])
+            nc.sync.dma_start(out=out[nt * P : (nt + 1) * P, :], in_=result[:])

@@ -1,3 +1,5 @@
+from contextlib import ExitStack
+
 import concourse.mybir as mybir
 from concourse.masks import make_identity
 
@@ -21,9 +23,10 @@ FEATURE_TILES = FEATURES // P
 H_PASSES = CHILDREN * FEATURES // K_PASS
 CHUNKS = CHILDREN * H_PASSES
 HALF = NODES // 2
+AGGR_TILES = CHILDREN * FEATURE_TILES
 
 RAW_BUFS = 10
-VECTOR_COLS = 192
+GPSIMD_COLS = 192
 RUN = 4
 
 FLOPS = 2 * NODES * (CHILDREN * FEATURES) ** 2 + 2 * NODES * FEATURES * FEATURES
@@ -35,20 +38,30 @@ def tile_treelstmcell_pa_kernel(
     nc = tc.nc
     hf = neighbour_h.rearrange("n c f -> n (c f)")
 
-    with tc.tile_pool(name="const", bufs=1) as const, tc.tile_pool(
-        name="raw", bufs=RAW_BUFS
-    ) as raw_pool, tc.tile_pool(name="stage", bufs=3) as stage, tc.tile_pool(
-        name="codes", bufs=2
-    ) as codes_pool, tc.tile_pool(name="work", bufs=3) as work, tc.psum_pool(
-        name="sums", bufs=1
-    ) as psum_sums, tc.psum_pool(name="acc", bufs=2) as psum_acc, tc.psum_pool(
-        name="flip", bufs=2
-    ) as psum_flip:
-        h_sb = []
-        for nt in range(NODE_TILES):
-            h_tile = const.tile([P, CHILDREN * FEATURES], BF16, name="h_sb%d" % nt)
-            nc.sync.dma_start(out=h_tile[:], in_=hf[nt * P : (nt + 1) * P, :])
-            h_sb.append(h_tile)
+    with ExitStack() as stack:
+        const = stack.enter_context(tc.tile_pool(name="const", bufs=1))
+        raw_pool = stack.enter_context(tc.tile_pool(name="raw", bufs=RAW_BUFS))
+        stage = stack.enter_context(tc.tile_pool(name="stage", bufs=3))
+        codes_pool = stack.enter_context(tc.tile_pool(name="codes", bufs=2))
+        work = stack.enter_context(tc.tile_pool(name="work", bufs=3))
+        psum_out = stack.enter_context(tc.psum_pool(name="psum_out", bufs=1))
+        psum_acc = stack.enter_context(tc.psum_pool(name="psum_acc", bufs=2))
+        psum_flip = stack.enter_context(tc.psum_pool(name="psum_flip", bufs=2))
+        stack.enter_context(tc.manual_schedule())
+
+        bias_rows = const.tile([P, P], BF16)
+        nc.vector.memset(bias_rows[:], 0.0)
+        nc.scalar.dma_start(
+            out=bias_rows[0:AGGR_TILES, :], in_=b_aggr_f.rearrange("(r m) -> r m", m=P)
+        )
+        nc.scalar.dma_start(
+            out=bias_rows[AGGR_TILES : AGGR_TILES + FEATURE_TILES, :],
+            in_=b_f_in.rearrange("(r m) -> r m", m=P),
+        )
+        mask_rows = const.tile([P, NODES], BF16)
+        nc.vector.memset(mask_rows[:], 0.0)
+        nc.scalar.dma_start(out=mask_rows[0:1, :], in_=x_mask.rearrange("(o n) -> o n", o=1))
+
         x_sb = const.tile([P, NODE_TILES * FEATURES], BF16)
         nc.sync.dma_start(
             out=x_sb[:].rearrange("p (t k) -> p t k", t=NODE_TILES),
@@ -56,6 +69,11 @@ def tile_treelstmcell_pa_kernel(
         )
         wf_raw = const.tile([P, PACK, FEATURES], BF16)
         nc.sync.dma_start(out=wf_raw[:], in_=W_f_in.rearrange("(p t) n -> p t n", t=PACK))
+        h_sb = []
+        for nt in range(NODE_TILES):
+            h_tile = const.tile([P, CHILDREN * FEATURES], BF16, name="h_sb%d" % nt)
+            nc.sync.dma_start(out=h_tile[:], in_=hf[nt * P : (nt + 1) * P, :])
+            h_sb.append(h_tile)
 
         raw_of = {}
         c_sb = {}
@@ -80,20 +98,6 @@ def tile_treelstmcell_pa_kernel(
         for chunk in range(RAW_BUFS):
             load_chunk(chunk)
 
-        bias_rows = const.tile([P, P], BF16)
-        nc.vector.memset(bias_rows[:], 0.0)
-        aggr_rows = CHILDREN * FEATURE_TILES
-        nc.scalar.dma_start(
-            out=bias_rows[0:aggr_rows, :], in_=b_aggr_f.rearrange("(r m) -> r m", m=P)
-        )
-        nc.scalar.dma_start(
-            out=bias_rows[aggr_rows : aggr_rows + FEATURE_TILES, :],
-            in_=b_f_in.rearrange("(r m) -> r m", m=P),
-        )
-        mask_rows = const.tile([P, NODES], BF16)
-        nc.vector.memset(mask_rows[:], 0.0)
-        nc.scalar.dma_start(out=mask_rows[0:1, :], in_=x_mask.rearrange("(o n) -> o n", o=1))
-
         ident_f32 = const.tile([P, P], F32)
         make_identity(nc, ident_f32[:])
         ident_bf = const.tile([P, P], BF16)
@@ -105,6 +109,75 @@ def tile_treelstmcell_pa_kernel(
         nc.vector.memset(warm[:], 0.0)
         nc.scalar.activation(out=warm[:, 1:2], in_=warm[:, 0:1], func=SIGMOID)
 
+        def quantise(grouped, codes, scales):
+            nc.vector.quantize_mx(out=codes.bitcast(FP8X4), scales=scales, in_=grouped)
+
+        def regroup(raw):
+            grouped = stage.tile([P, FEATURES, PACK], BF16, tag="grouped", align_bytes=64)
+            nc.gpsimd.tensor_scalar(
+                out=grouped[:, :GPSIMD_COLS, :],
+                in0=raw[:, :, :GPSIMD_COLS].rearrange("p t c -> p c t"),
+                scalar1=1.0,
+                scalar2=0.0,
+                op0=MULT,
+                op1=ADD,
+            )
+            nc.scalar.copy(
+                out=grouped[:, GPSIMD_COLS:, :].rearrange("p (c i) t -> p c t i", i=RUN),
+                in_=raw[:, :, GPSIMD_COLS:].rearrange("p t (c i) -> p c t i", i=RUN),
+            )
+            return grouped
+
+        x_codes = const.tile([P, NODES], U32, align_bytes=64)
+        x_scales = const.tile([P, NODES], U8, align_bytes=64)
+        h_codes = const.tile([P, H_PASSES, NODES], U32, align_bytes=64)
+        h_scales = const.tile([P, H_PASSES, NODES], U8, align_bytes=64)
+        wf_codes = const.tile([P, FEATURES], U32, align_bytes=64)
+        wf_scales = const.tile([P, FEATURES], U8, align_bytes=64)
+
+        def flip_half(words_of, half, step):
+            bank = psum_flip.tile([P, 2, HALF], F32, tag="flip")
+            for side in range(2):
+                pairs = words_of(2 * half + side).rearrange("n (p u) -> n u p", u=2)
+                for u in range(2):
+                    nc.tensor.transpose(
+                        bank[:, u, side * P : (side + 1) * P], pairs[:, u, :], ident_f32[:]
+                    )
+            grouped = stage.tile([P, HALF * PACK], BF16, tag="flipped", align_bytes=64)
+            words_out = grouped[:].bitcast(F32).rearrange("p (n u) -> p n u", u=2)
+            words_in = bank[:].rearrange("p u n -> p n u")
+            if step % 2 == 0:
+                nc.scalar.copy(out=words_out, in_=words_in)
+            else:
+                nc.vector.tensor_copy(out=words_out, in_=words_in)
+            return grouped
+
+        def flip_and_quantise(passes):
+            waiting = None
+            step = 0
+            for half in range(2):
+                nodes = slice(half * HALF, (half + 1) * HALF)
+                for words_of, codes, scales in passes:
+                    grouped = flip_half(words_of, half, step)
+                    if waiting is not None:
+                        quantise(*waiting)
+                    waiting = (grouped[:], codes[:, nodes], scales[:, nodes])
+                    step += 1
+            quantise(*waiting)
+
+        def x_words(nt):
+            return x_sb[:].bitcast(F32)[:, nt * K_PASS // 2 : (nt + 1) * K_PASS // 2]
+
+        def h_words(g):
+            return lambda nt: h_sb[nt][:].bitcast(F32)[:, g * K_PASS // 2 : (g + 1) * K_PASS // 2]
+
+        flip_and_quantise([(x_words, x_codes[:], x_scales[:])])
+        wf_grouped = regroup(wf_raw)
+        quantise(wf_grouped[:].rearrange("p c t -> p (c t)"), wf_codes[:], wf_scales[:])
+        flip_and_quantise(
+            [(h_words(g), h_codes[:, g, :], h_scales[:, g, :]) for g in range(H_PASSES)]
+        )
+
         bias_ps = psum_flip.tile([P, P], BF16, tag="flip")
         nc.tensor.transpose(bias_ps[:], bias_rows[:], ident_bf[:])
         bias_cols = const.tile([P, P], F32)
@@ -115,67 +188,9 @@ def tile_treelstmcell_pa_kernel(
         double_mask = const.tile([P, NODES], F32)
         nc.vector.tensor_copy(out=double_mask[:], in_=mask_ps[:])
 
-        h_codes = const.tile([P, H_PASSES, NODES], U32, align_bytes=64)
-        h_scales = const.tile([P, H_PASSES, NODES], U8, align_bytes=64)
-        x_codes = const.tile([P, NODES], U32, align_bytes=64)
-        x_scales = const.tile([P, NODES], U8, align_bytes=64)
+        input_term = {}
 
-        def flip_half(words_of, half):
-            bank = psum_flip.tile([P, 2, HALF], F32, tag="flip")
-            for side in range(2):
-                pairs = words_of(2 * half + side).rearrange("n (p u) -> n u p", u=2)
-                for u in range(2):
-                    nc.tensor.transpose(
-                        bank[:, u, side * P : (side + 1) * P], pairs[:, u, :], ident_f32[:]
-                    )
-            grouped = stage.tile([P, HALF * PACK], BF16, tag="flipped", align_bytes=64)
-            nc.scalar.copy(
-                out=grouped[:].bitcast(F32).rearrange("p (n u) -> p n u", u=2),
-                in_=bank[:].rearrange("p u n -> p n u"),
-            )
-            return grouped
-
-        def quantise(grouped, codes, scales):
-            nc.vector.quantize_mx(out=codes.bitcast(FP8X4), scales=scales, in_=grouped)
-
-        def h_words(g):
-            return lambda nt: h_sb[nt][:].bitcast(F32)[:, g * K_PASS // 2 : (g + 1) * K_PASS // 2]
-
-        def x_words(nt):
-            return x_sb[:].bitcast(F32)[:, nt * K_PASS // 2 : (nt + 1) * K_PASS // 2]
-
-        flips = []
-        for half in range(2):
-            for g in range(H_PASSES):
-                flips.append((h_words(g), half, h_codes[:, g, :], h_scales[:, g, :]))
-        for half in range(2):
-            flips.append((x_words, half, x_codes[:], x_scales[:]))
-
-        waiting = None
-        for words_of, half, codes, scales in flips:
-            grouped = flip_half(words_of, half)
-            if waiting is not None:
-                quantise(*waiting)
-            nodes = slice(half * HALF, (half + 1) * HALF)
-            waiting = (grouped[:], codes[:, nodes], scales[:, nodes])
-        quantise(*waiting)
-
-        def regroup(raw):
-            grouped = stage.tile([P, FEATURES, PACK], BF16, tag="grouped", align_bytes=64)
-            src = raw[:].rearrange("p t (c i) -> p c t i", i=RUN)
-            dst = grouped[:].rearrange("p (c i) t -> p c t i", i=RUN)
-            split = VECTOR_COLS // RUN
-            nc.vector.tensor_copy(out=dst[:, :split], in_=src[:, :split])
-            nc.scalar.copy(out=dst[:, split:], in_=src[:, split:])
-            return grouped
-
-        wf_codes = const.tile([P, FEATURES], U32, align_bytes=64)
-        wf_scales = const.tile([P, FEATURES], U8, align_bytes=64)
-        wf_grouped = regroup(wf_raw)
-        quantise(wf_grouped[:].rearrange("p c t -> p (c t)"), wf_codes[:], wf_scales[:])
-
-        input_term = []
-        for ft in range(FEATURE_TILES):
+        def make_input_term(ft):
             cols = slice(ft * P, (ft + 1) * P)
             fi_ps = psum_acc.tile([P, NODES], F32, tag="acc")
             nc.tensor.matmul_mx(
@@ -191,20 +206,22 @@ def tile_treelstmcell_pa_kernel(
             nc.vector.scalar_tensor_tensor(
                 out=term[:],
                 in0=fi_ps[:],
-                scalar=bias_cols[:, aggr_rows + ft : aggr_rows + ft + 1],
+                scalar=bias_cols[:, AGGR_TILES + ft : AGGR_TILES + ft + 1],
                 in1=double_mask[:],
                 op0=ADD,
                 op1=MULT,
             )
-            input_term.append(term)
+            input_term[ft] = term
 
         out_sums = [
-            psum_sums.tile([P, FEATURES], F32, name="out_sums%d" % nt) for nt in range(NODE_TILES)
+            psum_out.tile([P, NODE_TILES, P], F32, name="out_sums%d" % ft)
+            for ft in range(FEATURE_TILES)
         ]
         grouped_of = {}
         w_codes = {}
         w_scales = {}
         acc_of = {}
+        pre_of = {}
         gate_of = {}
         cells_t = {}
 
@@ -238,16 +255,19 @@ def tile_treelstmcell_pa_kernel(
                 )
             acc_of[(child, ft)] = acc
 
-        def squash(child, ft):
+        def add_input_term(child, ft):
             pre = work.tile([P, NODES], F32, tag="pre")
             nc.vector.tensor_tensor(
                 out=pre[:], in0=acc_of[(child, ft)][:], in1=input_term[ft][:], op=ADD
             )
+            pre_of[(child, ft)] = pre
+
+        def squash(child, ft):
             gate = work.tile([P, NODES], F32, tag="gate")
             tile_index = child * FEATURE_TILES + ft
             nc.scalar.activation(
                 out=gate[:],
-                in_=pre[:],
+                in_=pre_of[(child, ft)][:],
                 func=SIGMOID,
                 bias=bias_cols[:, tile_index : tile_index + 1],
                 scale=1.0,
@@ -276,42 +296,52 @@ def tile_treelstmcell_pa_kernel(
             )
             for nt in range(NODE_TILES):
                 nc.tensor.matmul(
-                    out=out_sums[nt][:, ft * P : (ft + 1) * P],
+                    out=out_sums[ft][:, nt, :],
                     lhsT=weighted[:, nt * P : (nt + 1) * P],
                     rhs=ident_f32[:],
                     is_transpose=True,
-                    start=(child == 0 and ft == 0),
-                    stop=(child == CHILDREN - 1 and ft == FEATURE_TILES - 1),
+                    start=(child == 0 and nt == 0),
+                    stop=(child == CHILDREN - 1 and nt == NODE_TILES - 1),
                 )
 
+        def store_out(ft):
+            result = work.tile([P, NODE_TILES, P], F32, tag="result")
+            if ft % 2 == 0:
+                nc.scalar.copy(out=result[:], in_=out_sums[ft][:])
+            else:
+                nc.vector.tensor_copy(out=result[:], in_=out_sums[ft][:])
+            nc.sync.dma_start(
+                out=out.rearrange("(t p) f -> p t f", p=P)[:, :, ft * P : (ft + 1) * P],
+                in_=result[:],
+            )
+
         def tile_at(slot, lag):
-            child, ft = divmod(slot - H_PASSES - lag, H_PASSES)
+            child, ft = divmod(slot - (H_PASSES + 1) - lag, H_PASSES)
             if 0 <= child < CHILDREN and ft < FEATURE_TILES:
                 return child, ft
             return None
 
-        STAGES = 3
-        for slot in range(CHUNKS + FEATURE_TILES + STAGES - 1):
+        LAST_LAG = 3
+        for slot in range(CHUNKS + 1 + FEATURE_TILES + LAST_LAG):
+            coming, entering, middle = tile_at(slot, -1), tile_at(slot, 0), tile_at(slot, 1)
+            leaving, summed = tile_at(slot, 2), tile_at(slot, LAST_LAG)
+            if slot < FEATURE_TILES:
+                make_input_term(slot)
+            if entering is not None:
+                multiply(*entering)
+            if middle is not None:
+                add_input_term(*middle)
+            if leaving is not None:
+                weigh_and_sum(*leaving)
+            if coming is not None and coming[1] % 2 == 0:
+                flip_cells(coming[0], coming[1] // 2)
             if slot < CHUNKS:
                 grouped_of[slot] = regroup(raw_of[slot])
             if slot + RAW_BUFS < CHUNKS:
                 load_chunk(slot + RAW_BUFS)
             if 1 <= slot <= CHUNKS:
                 quantise_chunk(slot - 1)
-            entering = tile_at(slot, 0)
-            if entering is not None:
-                multiply(*entering)
-            if tile_at(slot, 1) is not None:
-                squash(*tile_at(slot, 1))
-            if tile_at(slot, 2) is not None:
-                weigh_and_sum(*tile_at(slot, 2))
-            if entering is not None and entering[1] % 2 == 0:
-                flip_cells(entering[0], entering[1] // 2)
-
-        for nt in range(NODE_TILES):
-            result = work.tile([P, FEATURES], F32, tag="result")
-            if nt % 2 == 0:
-                nc.vector.tensor_copy(out=result[:], in_=out_sums[nt][:])
-            else:
-                nc.scalar.copy(out=result[:], in_=out_sums[nt][:])
-            nc.sync.dma_start(out=out[nt * P : (nt + 1) * P, :], in_=result[:])
+            if middle is not None:
+                squash(*middle)
+            if summed is not None and summed[0] == CHILDREN - 1:
+                store_out(summed[1])

@@ -26,7 +26,7 @@ HALF = NODES // 2
 AGGR_TILES = CHILDREN * FEATURE_TILES
 
 RAW_BUFS = 10
-GPSIMD_COLS = 192
+VECTOR_COLS = 144
 RUN = 4
 
 FLOPS = 2 * NODES * (CHILDREN * FEATURES) ** 2 + 2 * NODES * FEATURES * FEATURES
@@ -114,18 +114,11 @@ def tile_treelstmcell_pa_kernel(
 
         def regroup(raw):
             grouped = stage.tile([P, FEATURES, PACK], BF16, tag="grouped", align_bytes=64)
-            nc.gpsimd.tensor_scalar(
-                out=grouped[:, :GPSIMD_COLS, :],
-                in0=raw[:, :, :GPSIMD_COLS].rearrange("p t c -> p c t"),
-                scalar1=1.0,
-                scalar2=0.0,
-                op0=MULT,
-                op1=ADD,
-            )
-            nc.scalar.copy(
-                out=grouped[:, GPSIMD_COLS:, :].rearrange("p (c i) t -> p c t i", i=RUN),
-                in_=raw[:, :, GPSIMD_COLS:].rearrange("p t (c i) -> p c t i", i=RUN),
-            )
+            src = raw[:].rearrange("p t (c i) -> p c t i", i=RUN)
+            dst = grouped[:].rearrange("p (c i) t -> p c t i", i=RUN)
+            split = VECTOR_COLS // RUN
+            nc.vector.tensor_copy(out=dst[:, :split], in_=src[:, :split])
+            nc.scalar.copy(out=dst[:, split:], in_=src[:, split:])
             return grouped
 
         x_codes = const.tile([P, NODES], U32, align_bytes=64)

@@ -26,7 +26,7 @@ HALF = NODES // 2
 AGGR_TILES = CHILDREN * FEATURE_TILES
 
 RAW_BUFS = 10
-VECTOR_COLS = 144
+GPSIMD_COLS = 192
 RUN = 4
 
 FLOPS = 2 * NODES * (CHILDREN * FEATURES) ** 2 + 2 * NODES * FEATURES * FEATURES
@@ -47,7 +47,6 @@ def tile_treelstmcell_pa_kernel(
         psum_out = stack.enter_context(tc.psum_pool(name="psum_out", bufs=1))
         psum_acc = stack.enter_context(tc.psum_pool(name="psum_acc", bufs=2))
         psum_flip = stack.enter_context(tc.psum_pool(name="psum_flip", bufs=2))
-        stack.enter_context(tc.manual_schedule())
 
         bias_rows = const.tile([P, P], BF16)
         nc.vector.memset(bias_rows[:], 0.0)
@@ -114,11 +113,18 @@ def tile_treelstmcell_pa_kernel(
 
         def regroup(raw):
             grouped = stage.tile([P, FEATURES, PACK], BF16, tag="grouped", align_bytes=64)
-            src = raw[:].rearrange("p t (c i) -> p c t i", i=RUN)
-            dst = grouped[:].rearrange("p (c i) t -> p c t i", i=RUN)
-            split = VECTOR_COLS // RUN
-            nc.vector.tensor_copy(out=dst[:, :split], in_=src[:, :split])
-            nc.scalar.copy(out=dst[:, split:], in_=src[:, split:])
+            nc.gpsimd.tensor_scalar(
+                out=grouped[:, :GPSIMD_COLS, :],
+                in0=raw[:, :, :GPSIMD_COLS].rearrange("p t c -> p c t"),
+                scalar1=1.0,
+                scalar2=0.0,
+                op0=MULT,
+                op1=ADD,
+            )
+            nc.scalar.copy(
+                out=grouped[:, GPSIMD_COLS:, :].rearrange("p (c i) t -> p c t i", i=RUN),
+                in_=raw[:, :, GPSIMD_COLS:].rearrange("p t (c i) -> p c t i", i=RUN),
+            )
             return grouped
 
         x_codes = const.tile([P, NODES], U32, align_bytes=64)

@@ -26,7 +26,11 @@ HALF = NODES // 2
 AGGR_TILES = CHILDREN * FEATURE_TILES
 
 RAW_BUFS = 10
-GPSIMD_COLS = 192
+GPSIMD_COLS = 224
+FREE_V = 256
+FREE_G = 0
+HEAD_V = 128
+HEAD_G = 0
 RUN = 4
 
 FLOPS = 2 * NODES * (CHILDREN * FEATURES) ** 2 + 2 * NODES * FEATURES * FEATURES
@@ -48,18 +52,9 @@ def tile_treelstmcell_pa_kernel(
         psum_acc = stack.enter_context(tc.psum_pool(name="psum_acc", bufs=2))
         psum_flip = stack.enter_context(tc.psum_pool(name="psum_flip", bufs=2))
 
-        bias_rows = const.tile([P, P], BF16)
-        nc.vector.memset(bias_rows[:], 0.0)
-        nc.scalar.dma_start(
-            out=bias_rows[0:AGGR_TILES, :], in_=b_aggr_f.rearrange("(r m) -> r m", m=P)
-        )
-        nc.scalar.dma_start(
-            out=bias_rows[AGGR_TILES : AGGR_TILES + FEATURE_TILES, :],
-            in_=b_f_in.rearrange("(r m) -> r m", m=P),
-        )
-        mask_rows = const.tile([P, NODES], BF16)
-        nc.vector.memset(mask_rows[:], 0.0)
-        nc.scalar.dma_start(out=mask_rows[0:1, :], in_=x_mask.rearrange("(o n) -> o n", o=1))
+        warm = const.tile([P, 2], F32)
+        nc.vector.memset(warm[:], 0.0)
+        nc.scalar.activation(out=warm[:, 1:2], in_=warm[:, 0:1], func=SIGMOID)
 
         x_sb = const.tile([P, NODE_TILES * FEATURES], BF16)
         nc.sync.dma_start(
@@ -68,14 +63,28 @@ def tile_treelstmcell_pa_kernel(
         )
         wf_raw = const.tile([P, PACK, FEATURES], BF16)
         nc.sync.dma_start(out=wf_raw[:], in_=W_f_in.rearrange("(p t) n -> p t n", t=PACK))
+
+        bias_rows = const.tile([P, P], BF16)
+        nc.vector.memset(bias_rows[:], 0.0)
+        nc.sync.dma_start(
+            out=bias_rows[0:AGGR_TILES, :], in_=b_aggr_f.rearrange("(r m) -> r m", m=P)
+        )
+        nc.sync.dma_start(
+            out=bias_rows[AGGR_TILES : AGGR_TILES + FEATURE_TILES, :],
+            in_=b_f_in.rearrange("(r m) -> r m", m=P),
+        )
+        mask_rows = const.tile([P, NODES], BF16)
+        nc.vector.memset(mask_rows[:], 0.0)
+        nc.sync.dma_start(out=mask_rows[0:1, :], in_=x_mask.rearrange("(o n) -> o n", o=1))
+
         h_sb = []
-        for nt in range(NODE_TILES):
+        raw_of = {}
+        c_sb = {}
+
+        def load_nodes(nt):
             h_tile = const.tile([P, CHILDREN * FEATURES], BF16, name="h_sb%d" % nt)
             nc.sync.dma_start(out=h_tile[:], in_=hf[nt * P : (nt + 1) * P, :])
             h_sb.append(h_tile)
-
-        raw_of = {}
-        c_sb = {}
 
         def load_chunk(chunk):
             child, g = divmod(chunk, H_PASSES)
@@ -94,6 +103,8 @@ def tile_treelstmcell_pa_kernel(
                 )
                 c_sb[child] = cells
 
+        for nt in range(NODE_TILES):
+            load_nodes(nt)
         for chunk in range(RAW_BUFS):
             load_chunk(chunk)
 
@@ -104,26 +115,33 @@ def tile_treelstmcell_pa_kernel(
         twos = const.tile([P, P], BF16)
         nc.vector.memset(twos[:], 2.0)
 
-        warm = const.tile([P, 2], F32)
-        nc.vector.memset(warm[:], 0.0)
-        nc.scalar.activation(out=warm[:, 1:2], in_=warm[:, 0:1], func=SIGMOID)
-
         def quantise(grouped, codes, scales):
             nc.vector.quantize_mx(out=codes.bitcast(FP8X4), scales=scales, in_=grouped)
 
-        def regroup(raw):
+        def regroup(raw, vector_cols=0, gpsimd_cols=GPSIMD_COLS):
             grouped = stage.tile([P, FEATURES, PACK], BF16, tag="grouped", align_bytes=64)
-            nc.gpsimd.tensor_scalar(
-                out=grouped[:, :GPSIMD_COLS, :],
-                in0=raw[:, :, :GPSIMD_COLS].rearrange("p t c -> p c t"),
-                scalar1=1.0,
-                scalar2=0.0,
-                op0=MULT,
-                op1=ADD,
-            )
+            if gpsimd_cols:
+                nc.gpsimd.tensor_scalar(
+                    out=grouped[:, :gpsimd_cols, :],
+                    in0=raw[:, :, :gpsimd_cols].rearrange("p t c -> p c t"),
+                    scalar1=1.0,
+                    scalar2=0.0,
+                    op0=MULT,
+                    op1=ADD,
+                )
+            scalar_from = gpsimd_cols + vector_cols
+            if vector_cols:
+                nc.vector.tensor_copy(
+                    out=grouped[:, gpsimd_cols:scalar_from, :].rearrange(
+                        "p (c i) t -> p c t i", i=RUN
+                    ),
+                    in_=raw[:, :, gpsimd_cols:scalar_from].rearrange(
+                        "p t (c i) -> p c t i", i=RUN
+                    ),
+                )
             nc.scalar.copy(
-                out=grouped[:, GPSIMD_COLS:, :].rearrange("p (c i) t -> p c t i", i=RUN),
-                in_=raw[:, :, GPSIMD_COLS:].rearrange("p t (c i) -> p c t i", i=RUN),
+                out=grouped[:, scalar_from:, :].rearrange("p (c i) t -> p c t i", i=RUN),
+                in_=raw[:, :, scalar_from:].rearrange("p t (c i) -> p c t i", i=RUN),
             )
             return grouped
 
@@ -134,49 +152,63 @@ def tile_treelstmcell_pa_kernel(
         wf_codes = const.tile([P, FEATURES], U32, align_bytes=64)
         wf_scales = const.tile([P, FEATURES], U8, align_bytes=64)
 
-        def flip_half(words_of, half, step):
-            bank = psum_flip.tile([P, 2, HALF], F32, tag="flip")
-            for side in range(2):
-                pairs = words_of(2 * half + side).rearrange("n (p u) -> n u p", u=2)
+        out_sums = [
+            psum_out.tile([P, NODE_TILES, P], F32, name="out_sums%d" % ft)
+            for ft in range(FEATURE_TILES)
+        ]
+        flips = []
+
+        def flip_blocks(blocks):
+            step = len(flips)
+            flips.append(step)
+            bank = out_sums[step % FEATURE_TILES]
+            for j, (rows, codes, scales) in enumerate(blocks):
+                pairs = rows.rearrange("n (p u) -> n u p", u=2)
                 for u in range(2):
-                    nc.tensor.transpose(
-                        bank[:, u, side * P : (side + 1) * P], pairs[:, u, :], ident_f32[:]
-                    )
-            grouped = stage.tile([P, HALF * PACK], BF16, tag="flipped", align_bytes=64)
-            words_out = grouped[:].bitcast(F32).rearrange("p (n u) -> p n u", u=2)
-            words_in = bank[:].rearrange("p u n -> p n u")
-            if step % 2 == 0:
+                    nc.tensor.transpose(bank[:, 2 * j + u, :], pairs[:, u, :], ident_f32[:])
+            grouped = stage.tile([P, 2, P * PACK], BF16, tag="flipped", align_bytes=64)
+            used = len(blocks)
+            words_out = (
+                grouped[:, :used, :]
+                .rearrange("p j m -> p (j m)")
+                .bitcast(F32)
+                .rearrange("p (j n u) -> p j n u", j=used, u=2)
+            )
+            words_in = bank[:, : 2 * used, :].rearrange("p (j u) n -> p j n u", u=2)
+            if step % 3 != 2:
                 nc.scalar.copy(out=words_out, in_=words_in)
             else:
                 nc.vector.tensor_copy(out=words_out, in_=words_in)
-            return grouped
+            return [
+                (grouped[:, j, :], codes, scales) for j, (rows, codes, scales) in enumerate(blocks)
+            ]
 
-        def flip_and_quantise(passes):
-            waiting = None
-            step = 0
-            for half in range(2):
-                nodes = slice(half * HALF, (half + 1) * HALF)
-                for words_of, codes, scales in passes:
-                    grouped = flip_half(words_of, half, step)
-                    if waiting is not None:
-                        quantise(*waiting)
-                    waiting = (grouped[:], codes[:, nodes], scales[:, nodes])
-                    step += 1
-            quantise(*waiting)
+        def x_block(nt):
+            nodes = slice(nt * P, (nt + 1) * P)
+            words = x_sb[:].bitcast(F32)[:, nt * K_PASS // 2 : (nt + 1) * K_PASS // 2]
+            return words, x_codes[:, nodes], x_scales[:, nodes]
 
-        def x_words(nt):
-            return x_sb[:].bitcast(F32)[:, nt * K_PASS // 2 : (nt + 1) * K_PASS // 2]
+        def h_block(nt, g):
+            nodes = slice(nt * P, (nt + 1) * P)
+            words = h_sb[nt][:].bitcast(F32)[:, g * K_PASS // 2 : (g + 1) * K_PASS // 2]
+            return words, h_codes[:, g, nodes], h_scales[:, g, nodes]
 
-        def h_words(g):
-            return lambda nt: h_sb[nt][:].bitcast(F32)[:, g * K_PASS // 2 : (g + 1) * K_PASS // 2]
+        to_quantise = []
 
-        flip_and_quantise([(x_words, x_codes[:], x_scales[:])])
+        def flip_in_turn(blocks):
+            for first in range(0, len(blocks), 2):
+                flipped = flip_blocks(blocks[first : first + 2])
+                quantise_flipped()
+                to_quantise.extend(flipped)
+
+        def quantise_flipped():
+            for item in to_quantise:
+                quantise(*item)
+            to_quantise.clear()
+
+        flip_in_turn([x_block(nt) for nt in range(NODE_TILES)])
         wf_grouped = regroup(wf_raw)
-        quantise(wf_grouped[:].rearrange("p c t -> p (c t)"), wf_codes[:], wf_scales[:])
-        flip_and_quantise(
-            [(h_words(g), h_codes[:, g, :], h_scales[:, g, :]) for g in range(H_PASSES)]
-        )
-
+        quantise_flipped()
         bias_ps = psum_flip.tile([P, P], BF16, tag="flip")
         nc.tensor.transpose(bias_ps[:], bias_rows[:], ident_bf[:])
         bias_cols = const.tile([P, P], F32)
@@ -187,13 +219,20 @@ def tile_treelstmcell_pa_kernel(
         double_mask = const.tile([P, NODES], F32)
         nc.vector.tensor_copy(out=double_mask[:], in_=mask_ps[:])
 
+
+        for nt in range(NODE_TILES):
+            flip_in_turn([h_block(nt, g) for g in range(H_PASSES)])
+            if nt == 0:
+                quantise(wf_grouped[:].rearrange("p c t -> p (c t)"), wf_codes[:], wf_scales[:])
+        quantise_flipped()
+
         input_term = {}
 
         def make_input_term(ft):
             cols = slice(ft * P, (ft + 1) * P)
-            fi_ps = psum_acc.tile([P, NODES], F32, tag="acc")
+            fi_ps = out_sums[ft][:].rearrange("p t n -> p (t n)")
             nc.tensor.matmul_mx(
-                out=fi_ps[:],
+                out=fi_ps,
                 lhsT=wf_codes[:, cols].bitcast(FP8X4),
                 lhsT_scale=wf_scales[:, cols],
                 rhs=x_codes[:].bitcast(FP8X4),
@@ -204,7 +243,7 @@ def tile_treelstmcell_pa_kernel(
             term = const.tile([P, NODES], F32, name="input_term%d" % ft)
             nc.vector.scalar_tensor_tensor(
                 out=term[:],
-                in0=fi_ps[:],
+                in0=fi_ps,
                 scalar=bias_cols[:, AGGR_TILES + ft : AGGR_TILES + ft + 1],
                 in1=double_mask[:],
                 op0=ADD,
@@ -212,16 +251,14 @@ def tile_treelstmcell_pa_kernel(
             )
             input_term[ft] = term
 
-        out_sums = [
-            psum_out.tile([P, NODE_TILES, P], F32, name="out_sums%d" % ft)
-            for ft in range(FEATURE_TILES)
-        ]
+
         grouped_of = {}
         w_codes = {}
         w_scales = {}
         acc_of = {}
         pre_of = {}
         gate_of = {}
+        weighted_of = {}
         cells_t = {}
 
         def quantise_chunk(chunk):
@@ -239,20 +276,30 @@ def tile_treelstmcell_pa_kernel(
                 w_scales[child][:, g, :],
             )
 
-        def multiply(child, ft):
+        def one_pass(child, ft, g):
             cols = slice(ft * P, (ft + 1) * P)
-            acc = psum_acc.tile([P, NODES], F32, tag="acc")
-            for g in range(H_PASSES):
-                nc.tensor.matmul_mx(
-                    out=acc[:],
-                    lhsT=w_codes[child][:, g, cols].bitcast(FP8X4),
-                    lhsT_scale=w_scales[child][:, g, cols],
-                    rhs=h_codes[:, g, :].bitcast(FP8X4),
-                    rhs_scale=h_scales[:, g, :],
-                    start=(g == 0),
-                    stop=(g == H_PASSES - 1),
-                )
-            acc_of[(child, ft)] = acc
+            nc.tensor.matmul_mx(
+                out=acc_of[(child, ft)][:],
+                lhsT=w_codes[child][:, g, cols].bitcast(FP8X4),
+                lhsT_scale=w_scales[child][:, g, cols],
+                rhs=h_codes[:, g, :].bitcast(FP8X4),
+                rhs_scale=h_scales[:, g, :],
+                start=(g == 0),
+                stop=(g == H_PASSES - 1),
+            )
+
+        def multiply_chunk(child, g):
+            for ft in range(FEATURE_TILES):
+                if g == 0:
+                    pool, tag = (psum_flip, "flip") if ft < 2 else (psum_acc, "acc")
+                    acc_of[(child, ft)] = pool.tile([P, NODES], F32, tag=tag, name="acc_first")
+                one_pass(child, ft, g)
+
+        def multiply(child, ft, passes=range(H_PASSES)):
+            if 0 in passes:
+                acc_of[(child, ft)] = psum_acc.tile([P, NODES], F32, tag="acc", name="acc")
+            for g in passes:
+                one_pass(child, ft, g)
 
         def add_input_term(child, ft):
             pre = work.tile([P, NODES], F32, tag="pre")
@@ -285,7 +332,7 @@ def tile_treelstmcell_pa_kernel(
                     )
             cells_t[(child, pair)] = bank
 
-        def weigh_and_sum(child, ft):
+        def weigh(child, ft):
             weighted = work.tile([P, NODES], F32, tag="weighted")
             nc.vector.tensor_tensor(
                 out=weighted[:],
@@ -293,6 +340,10 @@ def tile_treelstmcell_pa_kernel(
                 in1=cells_t[(child, ft // 2)][:, ft % 2, :],
                 op=MULT,
             )
+            weighted_of[(child, ft)] = weighted
+
+        def sum_up(child, ft):
+            weighted = weighted_of[(child, ft)]
             for nt in range(NODE_TILES):
                 nc.tensor.matmul(
                     out=out_sums[ft][:, nt, :],
@@ -304,7 +355,7 @@ def tile_treelstmcell_pa_kernel(
                 )
 
         def store_out(ft):
-            result = work.tile([P, NODE_TILES, P], F32, tag="result")
+            result = work.tile([P, NODE_TILES, P], F32, tag="result", bufs=4)
             if ft % 2 == 0:
                 nc.scalar.copy(out=result[:], in_=out_sums[ft][:])
             else:
@@ -320,27 +371,52 @@ def tile_treelstmcell_pa_kernel(
                 return child, ft
             return None
 
-        LAST_LAG = 3
-        for slot in range(CHUNKS + 1 + FEATURE_TILES + LAST_LAG):
-            coming, entering, middle = tile_at(slot, -1), tile_at(slot, 0), tile_at(slot, 1)
-            leaving, summed = tile_at(slot, 2), tile_at(slot, LAST_LAG)
-            if slot < FEATURE_TILES:
-                make_input_term(slot)
-            if entering is not None:
+        for slot in range(CHUNKS + 1):
+            entering, middle, leaving, summed = [tile_at(slot, lag) for lag in range(4)]
+            if slot < CHUNKS:
+                if slot < H_PASSES:
+                    grouped_of[slot] = regroup(raw_of[slot], HEAD_V, HEAD_G)
+                elif middle is None:
+                    grouped_of[slot] = regroup(raw_of[slot], FREE_V, FREE_G)
+                else:
+                    grouped_of[slot] = regroup(raw_of[slot])
+            if slot + RAW_BUFS < CHUNKS:
+                load_chunk(slot + RAW_BUFS)
+            if 1 <= slot <= FEATURE_TILES:
+                make_input_term(slot - 1)
+            if slot >= 1:
+                quantise_chunk(slot - 1)
+                if slot <= H_PASSES:
+                    multiply_chunk(0, slot - 1)
+            if entering is not None and entering[0] > 0:
                 multiply(*entering)
             if middle is not None:
                 add_input_term(*middle)
+            if summed is not None:
+                sum_up(*summed)
             if leaving is not None:
-                weigh_and_sum(*leaving)
-            if coming is not None and coming[1] % 2 == 0:
-                flip_cells(coming[0], coming[1] // 2)
-            if slot < CHUNKS:
-                grouped_of[slot] = regroup(raw_of[slot])
-            if slot + RAW_BUFS < CHUNKS:
-                load_chunk(slot + RAW_BUFS)
-            if 1 <= slot <= CHUNKS:
-                quantise_chunk(slot - 1)
+                weigh(*leaving)
             if middle is not None:
                 squash(*middle)
-            if summed is not None and summed[0] == CHILDREN - 1:
-                store_out(summed[1])
+            if middle is not None and middle[1] % 2 == 0:
+                flip_cells(middle[0], middle[1] // 2)
+        last = CHILDREN - 1
+        for step in range(FEATURE_TILES + 4):
+            if step < FEATURE_TILES:
+                multiply(last, step)
+            if step == 0:
+                sum_up(last - 1, 2)
+                weigh(last - 1, 3)
+                flip_cells(last, 0)
+            if step == 1:
+                sum_up(last - 1, 3)
+            if step == 2:
+                flip_cells(last, 1)
+            if step < FEATURE_TILES:
+                add_input_term(last, step)
+                squash(last, step)
+            if 1 <= step <= FEATURE_TILES:
+                weigh(last, step - 1)
+            if 2 <= step <= FEATURE_TILES + 1:
+                sum_up(last, step - 2)
+                store_out(step - 2)

@@ -27,10 +27,18 @@ AGGR_TILES = CHILDREN * FEATURE_TILES
 
 RAW_BUFS = 10
 GPSIMD_COLS = 224
-FREE_V = 256
-FREE_G = 0
-HEAD_V = 128
-HEAD_G = 0
+CELLS_BEHIND = 1
+STT_AT = 5
+HEAD_SLOTS = 5
+VE = 5
+W_AT = 4
+FI_AT = 3
+FLIPPED_BUFS = 6
+GROUPED_BUFS = 3
+SUM_LAG = 4
+SUM_EARLY = True
+HEAD_SHARES = (224, 0)
+SHARES = ((0, 224), (96, 112), (112, 112), (0, 224), (0, 224))
 RUN = 4
 
 FLOPS = 2 * NODES * (CHILDREN * FEATURES) ** 2 + 2 * NODES * FEATURES * FEATURES
@@ -51,6 +59,7 @@ def tile_treelstmcell_pa_kernel(
         psum_out = stack.enter_context(tc.psum_pool(name="psum_out", bufs=1))
         psum_acc = stack.enter_context(tc.psum_pool(name="psum_acc", bufs=2))
         psum_flip = stack.enter_context(tc.psum_pool(name="psum_flip", bufs=2))
+        stack.enter_context(tc.manual_schedule())
 
         warm = const.tile([P, 2], F32)
         nc.vector.memset(warm[:], 0.0)
@@ -86,6 +95,13 @@ def tile_treelstmcell_pa_kernel(
             nc.sync.dma_start(out=h_tile[:], in_=hf[nt * P : (nt + 1) * P, :])
             h_sb.append(h_tile)
 
+        def load_cells(child):
+            cells = const.tile([P, NODE_TILES, FEATURES], BF16, name="c_sb%d" % child)
+            nc.sync.dma_start(
+                out=cells[:], in_=neighbour_c[:, child, :].rearrange("(t p) f -> p t f", p=P)
+            )
+            c_sb[child] = cells
+
         def load_chunk(chunk):
             child, g = divmod(chunk, H_PASSES)
             raw = raw_pool.tile([P, PACK, FEATURES], BF16, tag="raw")
@@ -96,16 +112,14 @@ def tile_treelstmcell_pa_kernel(
                 ].rearrange("(p t) n -> p t n", t=PACK),
             )
             raw_of[chunk] = raw
-            if g == H_PASSES - 1:
-                cells = const.tile([P, NODE_TILES, FEATURES], BF16, name="c_sb%d" % child)
-                nc.sync.dma_start(
-                    out=cells[:], in_=neighbour_c[:, child, :].rearrange("(t p) f -> p t f", p=P)
-                )
-                c_sb[child] = cells
+            if g == CELLS_BEHIND and child > 0:
+                load_cells(child - 1)
 
         for nt in range(NODE_TILES):
+            if nt >= W_AT:
+                load_chunk(nt - W_AT)
             load_nodes(nt)
-        for chunk in range(RAW_BUFS):
+        for chunk in range(NODE_TILES - W_AT, RAW_BUFS):
             load_chunk(chunk)
 
         ident_f32 = const.tile([P, P], F32)
@@ -118,8 +132,9 @@ def tile_treelstmcell_pa_kernel(
         def quantise(grouped, codes, scales):
             nc.vector.quantize_mx(out=codes.bitcast(FP8X4), scales=scales, in_=grouped)
 
-        def regroup(raw, vector_cols=0, gpsimd_cols=GPSIMD_COLS):
-            grouped = stage.tile([P, FEATURES, PACK], BF16, tag="grouped", align_bytes=64)
+        def regroup_gs(raw, vector_cols, gpsimd_cols):
+            grouped = stage.tile([P, FEATURES, PACK], BF16, tag="grouped", bufs=GROUPED_BUFS, align_bytes=64)
+            scalar_from = gpsimd_cols + vector_cols
             if gpsimd_cols:
                 nc.gpsimd.tensor_scalar(
                     out=grouped[:, :gpsimd_cols, :],
@@ -129,21 +144,19 @@ def tile_treelstmcell_pa_kernel(
                     op0=MULT,
                     op1=ADD,
                 )
-            scalar_from = gpsimd_cols + vector_cols
-            if vector_cols:
-                nc.vector.tensor_copy(
-                    out=grouped[:, gpsimd_cols:scalar_from, :].rearrange(
-                        "p (c i) t -> p c t i", i=RUN
-                    ),
-                    in_=raw[:, :, gpsimd_cols:scalar_from].rearrange(
-                        "p t (c i) -> p c t i", i=RUN
-                    ),
-                )
             nc.scalar.copy(
                 out=grouped[:, scalar_from:, :].rearrange("p (c i) t -> p c t i", i=RUN),
                 in_=raw[:, :, scalar_from:].rearrange("p t (c i) -> p c t i", i=RUN),
             )
             return grouped
+
+        def regroup_v(raw, grouped, vector_cols, gpsimd_cols):
+            if vector_cols:
+                cols = slice(gpsimd_cols, gpsimd_cols + vector_cols)
+                nc.vector.tensor_copy(
+                    out=grouped[:, cols, :].rearrange("p (c i) t -> p c t i", i=RUN),
+                    in_=raw[:, :, cols].rearrange("p t (c i) -> p c t i", i=RUN),
+                )
 
         x_codes = const.tile([P, NODES], U32, align_bytes=64)
         x_scales = const.tile([P, NODES], U8, align_bytes=64)
@@ -166,7 +179,7 @@ def tile_treelstmcell_pa_kernel(
                 pairs = rows.rearrange("n (p u) -> n u p", u=2)
                 for u in range(2):
                     nc.tensor.transpose(bank[:, 2 * j + u, :], pairs[:, u, :], ident_f32[:])
-            grouped = stage.tile([P, 2, P * PACK], BF16, tag="flipped", align_bytes=64)
+            grouped = stage.tile([P, 2, P * PACK], BF16, tag="flipped", bufs=FLIPPED_BUFS, align_bytes=64)
             used = len(blocks)
             words_out = (
                 grouped[:, :used, :]
@@ -175,7 +188,7 @@ def tile_treelstmcell_pa_kernel(
                 .rearrange("p (j n u) -> p j n u", j=used, u=2)
             )
             words_in = bank[:, : 2 * used, :].rearrange("p (j u) n -> p j n u", u=2)
-            if step % 3 != 2:
+            if step % VE != VE - 1:
                 nc.scalar.copy(out=words_out, in_=words_in)
             else:
                 nc.vector.tensor_copy(out=words_out, in_=words_in)
@@ -207,7 +220,7 @@ def tile_treelstmcell_pa_kernel(
             to_quantise.clear()
 
         flip_in_turn([x_block(nt) for nt in range(NODE_TILES)])
-        wf_grouped = regroup(wf_raw)
+        wf_grouped = regroup_gs(wf_raw, 0, 224)
         quantise_flipped()
         bias_ps = psum_flip.tile([P, P], BF16, tag="flip")
         nc.tensor.transpose(bias_ps[:], bias_rows[:], ident_bf[:])
@@ -220,19 +233,14 @@ def tile_treelstmcell_pa_kernel(
         nc.vector.tensor_copy(out=double_mask[:], in_=mask_ps[:])
 
 
-        for nt in range(NODE_TILES):
-            flip_in_turn([h_block(nt, g) for g in range(H_PASSES)])
-            if nt == 0:
-                quantise(wf_grouped[:].rearrange("p c t -> p (c t)"), wf_codes[:], wf_scales[:])
-        quantise_flipped()
-
         input_term = {}
+        input_products = {}
 
-        def make_input_term(ft):
+        def multiply_input(ft):
             cols = slice(ft * P, (ft + 1) * P)
-            fi_ps = out_sums[ft][:].rearrange("p t n -> p (t n)")
+            product = out_sums[ft][:].rearrange("p t n -> p (t n)")
             nc.tensor.matmul_mx(
-                out=fi_ps,
+                out=product,
                 lhsT=wf_codes[:, cols].bitcast(FP8X4),
                 lhsT_scale=wf_scales[:, cols],
                 rhs=x_codes[:].bitcast(FP8X4),
@@ -240,10 +248,13 @@ def tile_treelstmcell_pa_kernel(
                 start=True,
                 stop=True,
             )
+            input_products[ft] = product
+
+        def finish_input_term(ft):
             term = const.tile([P, NODES], F32, name="input_term%d" % ft)
             nc.vector.scalar_tensor_tensor(
                 out=term[:],
-                in0=fi_ps,
+                in0=input_products[ft],
                 scalar=bias_cols[:, AGGR_TILES + ft : AGGR_TILES + ft + 1],
                 in1=double_mask[:],
                 op0=ADD,
@@ -251,8 +262,20 @@ def tile_treelstmcell_pa_kernel(
             )
             input_term[ft] = term
 
-
         grouped_of = {}
+        for nt in range(NODE_TILES):
+            if nt >= W_AT:
+                grouped_of[nt - W_AT] = regroup_gs(raw_of[nt - W_AT], *HEAD_SHARES)
+                regroup_v(raw_of[nt - W_AT], grouped_of[nt - W_AT], *HEAD_SHARES)
+            flip_in_turn([h_block(nt, g) for g in range(H_PASSES)])
+            if nt == FI_AT:
+                for ft in range(FEATURE_TILES):
+                    multiply_input(ft)
+            if nt == 0:
+                quantise(wf_grouped[:].rearrange("p c t -> p (c t)"), wf_codes[:], wf_scales[:])
+        quantise_flipped()
+
+
         w_codes = {}
         w_scales = {}
         acc_of = {}
@@ -366,57 +389,86 @@ def tile_treelstmcell_pa_kernel(
             )
 
         def tile_at(slot, lag):
-            child, ft = divmod(slot - (H_PASSES + 1) - lag, H_PASSES)
+            child, ft = divmod(slot - H_PASSES - lag, H_PASSES)
             if 0 <= child < CHILDREN and ft < FEATURE_TILES:
                 return child, ft
             return None
 
-        for slot in range(CHUNKS + 1):
-            entering, middle, leaving, summed = [tile_at(slot, lag) for lag in range(4)]
+        LAST = CHILDREN - 1
+        for slot in range(CHUNKS):
+            child, place = divmod(slot - H_PASSES, H_PASSES)
+            first, middle, leaving = [tile_at(slot, lag) for lag in (0, 2, 3)]
             if slot < CHUNKS:
-                if slot < H_PASSES:
-                    grouped_of[slot] = regroup(raw_of[slot], HEAD_V, HEAD_G)
-                elif middle is None:
-                    grouped_of[slot] = regroup(raw_of[slot], FREE_V, FREE_G)
+                shares = HEAD_SHARES if slot < HEAD_SLOTS else SHARES[place]
+                grouped_of[slot] = regroup_gs(raw_of[slot], *shares)
+            if STT_AT <= slot < STT_AT + 2:
+                for ft in range(2):
+                    finish_input_term(2 * (slot - STT_AT) + ft)
+            if middle is not None:
+                add_input_term(*middle)
+            if leaving is not None:
+                weigh(*leaving)
+            if slot == CHUNKS - 1:
+                multiply(LAST, 0, range(3))
+            if place == 2:
+                if child > 0:
+                    sum_up(child - 1, 2)
+                    sum_up(child - 1, 3)
+                if child >= 0:
+                    flip_cells(child, 0)
+            if place == 4 and child >= 0:
+                sum_up(child, 0)
+                sum_up(child, 1)
+                flip_cells(child, 1)
+            if slot == CHUNKS - 1:
+                flip_cells(LAST, 0)
+            if first is not None and 0 < child < LAST:
+                if place == 0:
+                    multiply(child, 0, range(H_PASSES - 1))
                 else:
-                    grouped_of[slot] = regroup(raw_of[slot])
+                    if place == 1:
+                        multiply(child, 0, [H_PASSES - 1])
+                    multiply(child, place)
+            if slot < CHUNKS:
+                regroup_v(raw_of[slot], grouped_of[slot], *shares)
             if slot + RAW_BUFS < CHUNKS:
                 load_chunk(slot + RAW_BUFS)
-            if 1 <= slot <= FEATURE_TILES:
-                make_input_term(slot - 1)
+            if slot + RAW_BUFS == CHUNKS:
+                load_cells(LAST)
             if slot >= 1:
                 quantise_chunk(slot - 1)
                 if slot <= H_PASSES:
                     multiply_chunk(0, slot - 1)
-            if entering is not None and entering[0] > 0:
-                multiply(*entering)
-            if middle is not None:
-                add_input_term(*middle)
-            if summed is not None:
-                sum_up(*summed)
-            if leaving is not None:
-                weigh(*leaving)
             if middle is not None:
                 squash(*middle)
-            if middle is not None and middle[1] % 2 == 0:
-                flip_cells(middle[0], middle[1] // 2)
-        last = CHILDREN - 1
-        for step in range(FEATURE_TILES + 4):
-            if step < FEATURE_TILES:
-                multiply(last, step)
-            if step == 0:
-                sum_up(last - 1, 2)
-                weigh(last - 1, 3)
-                flip_cells(last, 0)
-            if step == 1:
-                sum_up(last - 1, 3)
-            if step == 2:
-                flip_cells(last, 1)
-            if step < FEATURE_TILES:
-                add_input_term(last, step)
-                squash(last, step)
-            if 1 <= step <= FEATURE_TILES:
-                weigh(last, step - 1)
-            if 2 <= step <= FEATURE_TILES + 1:
-                sum_up(last, step - 2)
-                store_out(step - 2)
+        quantise_chunk(CHUNKS - 1)
+        multiply(LAST, 0, range(3, H_PASSES))
+        add_input_term(LAST - 1, 3)
+        squash(LAST - 1, 3)
+        multiply(LAST, 1)
+        add_input_term(LAST, 0)
+        squash(LAST, 0)
+        weigh(LAST - 1, 2)
+        multiply(LAST, 2)
+        add_input_term(LAST, 1)
+        squash(LAST, 1)
+        weigh(LAST - 1, 3)
+        multiply(LAST, 3)
+        flip_cells(LAST, 1)
+        sum_up(LAST - 1, 2)
+        sum_up(LAST - 1, 3)
+        weigh(LAST, 0)
+        add_input_term(LAST, 2)
+        squash(LAST, 2)
+        weigh(LAST, 1)
+        sum_up(LAST, 0)
+        sum_up(LAST, 1)
+        add_input_term(LAST, 3)
+        squash(LAST, 3)
+        weigh(LAST, 2)
+        sum_up(LAST, 2)
+        store_out(0)
+        weigh(LAST, 3)
+        sum_up(LAST, 3)
+        for ft in range(1, FEATURE_TILES):
+            store_out(ft)

@@ -28,17 +28,20 @@ AGGR_TILES = CHILDREN * FEATURE_TILES
 RAW_BUFS = 10
 GPSIMD_COLS = 224
 CELLS_BEHIND = 1
+S_ALL = True
+GATE = True
+GATE_FROM = 5
 STT_AT = 5
 HEAD_SLOTS = 5
 VE = 5
 W_AT = 4
 FI_AT = 3
 FLIPPED_BUFS = 6
-GROUPED_BUFS = 3
+GROUPED_BUFS = 4
 SUM_LAG = 4
 SUM_EARLY = True
 HEAD_SHARES = (224, 0)
-SHARES = ((0, 224), (96, 112), (112, 112), (0, 224), (0, 224))
+SHARES = ((0, 192), (96, 80), (96, 80), (0, 192), (0, 192))
 RUN = 4
 
 FLOPS = 2 * NODES * (CHILDREN * FEATURES) ** 2 + 2 * NODES * FEATURES * FEATURES
@@ -55,7 +58,7 @@ def tile_treelstmcell_pa_kernel(
         raw_pool = stack.enter_context(tc.tile_pool(name="raw", bufs=RAW_BUFS))
         stage = stack.enter_context(tc.tile_pool(name="stage", bufs=3))
         codes_pool = stack.enter_context(tc.tile_pool(name="codes", bufs=2))
-        work = stack.enter_context(tc.tile_pool(name="work", bufs=3))
+        work = stack.enter_context(tc.tile_pool(name="work", bufs=5))
         psum_out = stack.enter_context(tc.psum_pool(name="psum_out", bufs=1))
         psum_acc = stack.enter_context(tc.psum_pool(name="psum_acc", bufs=2))
         psum_flip = stack.enter_context(tc.psum_pool(name="psum_flip", bufs=2))
@@ -284,6 +287,12 @@ def tile_treelstmcell_pa_kernel(
         weighted_of = {}
         cells_t = {}
 
+        gate_word = const.tile([P, 1], U32)
+
+        def hold_gpsimd(chunk):
+            child, g = divmod(chunk, H_PASSES)
+            nc.gpsimd.tensor_copy(out=gate_word[:], in_=w_codes[child][:, g, 0:1])
+
         def quantise_chunk(chunk):
             child, g = divmod(chunk, H_PASSES)
             if g == 0:
@@ -379,7 +388,7 @@ def tile_treelstmcell_pa_kernel(
 
         def store_out(ft):
             result = work.tile([P, NODE_TILES, P], F32, tag="result", bufs=4)
-            if ft % 2 == 0:
+            if ft % 2 == 0 or S_ALL:
                 nc.scalar.copy(out=result[:], in_=out_sums[ft][:])
             else:
                 nc.vector.tensor_copy(out=result[:], in_=out_sums[ft][:])
@@ -400,16 +409,18 @@ def tile_treelstmcell_pa_kernel(
             first, middle, leaving = [tile_at(slot, lag) for lag in (0, 2, 3)]
             if slot < CHUNKS:
                 shares = HEAD_SHARES if slot < HEAD_SLOTS else SHARES[place]
+                if GATE and slot >= GATE_FROM and shares[1]:
+                    hold_gpsimd(slot - 2)
                 grouped_of[slot] = regroup_gs(raw_of[slot], *shares)
             if STT_AT <= slot < STT_AT + 2:
                 for ft in range(2):
                     finish_input_term(2 * (slot - STT_AT) + ft)
             if middle is not None:
                 add_input_term(*middle)
-            if leaving is not None:
-                weigh(*leaving)
             if slot == CHUNKS - 1:
                 multiply(LAST, 0, range(3))
+            if leaving is not None:
+                weigh(*leaving)
             if place == 2:
                 if child > 0:
                     sum_up(child - 1, 2)
@@ -421,7 +432,8 @@ def tile_treelstmcell_pa_kernel(
                 sum_up(child, 1)
                 flip_cells(child, 1)
             if slot == CHUNKS - 1:
-                flip_cells(LAST, 0)
+                add_input_term(LAST - 1, 3)
+                multiply(LAST, 1, range(3))
             if first is not None and 0 < child < LAST:
                 if place == 0:
                     multiply(child, 0, range(H_PASSES - 1))
@@ -441,17 +453,15 @@ def tile_treelstmcell_pa_kernel(
                     multiply_chunk(0, slot - 1)
             if middle is not None:
                 squash(*middle)
-        quantise_chunk(CHUNKS - 1)
-        multiply(LAST, 0, range(3, H_PASSES))
-        add_input_term(LAST - 1, 3)
         squash(LAST - 1, 3)
-        multiply(LAST, 1)
-        add_input_term(LAST, 0)
-        squash(LAST, 0)
+        quantise_chunk(CHUNKS - 1)
+        for ft in range(2):
+            multiply(LAST, ft, range(3, H_PASSES))
+            add_input_term(LAST, ft)
+            squash(LAST, ft)
+        flip_cells(LAST, 0)
         weigh(LAST - 1, 2)
         multiply(LAST, 2)
-        add_input_term(LAST, 1)
-        squash(LAST, 1)
         weigh(LAST - 1, 3)
         multiply(LAST, 3)
         flip_cells(LAST, 1)
@@ -461,14 +471,15 @@ def tile_treelstmcell_pa_kernel(
         add_input_term(LAST, 2)
         squash(LAST, 2)
         weigh(LAST, 1)
-        sum_up(LAST, 0)
-        sum_up(LAST, 1)
         add_input_term(LAST, 3)
         squash(LAST, 3)
+        sum_up(LAST, 0)
+        sum_up(LAST, 1)
+        store_out(0)
+        store_out(1)
         weigh(LAST, 2)
         sum_up(LAST, 2)
-        store_out(0)
+        store_out(2)
         weigh(LAST, 3)
         sum_up(LAST, 3)
-        for ft in range(1, FEATURE_TILES):
-            store_out(ft)
+        store_out(3)

@@ -42,7 +42,7 @@ SUM_LAG = 4
 SUM_EARLY = True
 HEAD_SHARES = (224, 0)
 SHARES = ((0, 192), (96, 80), (96, 80), (0, 192), (0, 192))
-RUN = 4
+RUN = 8
 
 FLOPS = 2 * NODES * (CHILDREN * FEATURES) ** 2 + 2 * NODES * FEATURES * FEATURES
 

@@ -28,7 +28,7 @@ AGGR_TILES = CHILDREN * FEATURE_TILES
 RAW_BUFS = 10
 GPSIMD_COLS = 224
 CELLS_BEHIND = 1
-S_ALL = True
+S_OUT = (0, 1, 2)
 GATE = True
 GATE_FROM = 5
 STT_AT = 5
@@ -365,7 +365,7 @@ def tile_treelstmcell_pa_kernel(
             cells_t[(child, pair)] = bank
 
         def weigh(child, ft):
-            weighted = work.tile([P, NODES], F32, tag="weighted")
+            weighted = work.tile([P, NODES], F32, tag="weighted", bufs=8)
             nc.vector.tensor_tensor(
                 out=weighted[:],
                 in0=gate_of[(child, ft)][:],
@@ -388,7 +388,7 @@ def tile_treelstmcell_pa_kernel(
 
         def store_out(ft):
             result = work.tile([P, NODE_TILES, P], F32, tag="result", bufs=4)
-            if ft % 2 == 0 or S_ALL:
+            if ft in S_OUT:
                 nc.scalar.copy(out=result[:], in_=out_sums[ft][:])
             else:
                 nc.vector.tensor_copy(out=result[:], in_=out_sums[ft][:])
@@ -428,8 +428,9 @@ def tile_treelstmcell_pa_kernel(
                 if child >= 0:
                     flip_cells(child, 0)
             if place == 4 and child >= 0:
-                sum_up(child, 0)
-                sum_up(child, 1)
+                if slot < CHUNKS - 1:
+                    sum_up(child, 0)
+                    sum_up(child, 1)
                 flip_cells(child, 1)
             if slot == CHUNKS - 1:
                 add_input_term(LAST - 1, 3)
@@ -457,25 +458,27 @@ def tile_treelstmcell_pa_kernel(
         quantise_chunk(CHUNKS - 1)
         for ft in range(2):
             multiply(LAST, ft, range(3, H_PASSES))
+        flip_cells(LAST, 0)
+        for ft in range(2):
             add_input_term(LAST, ft)
             squash(LAST, ft)
-        flip_cells(LAST, 0)
         weigh(LAST - 1, 2)
         multiply(LAST, 2)
         weigh(LAST - 1, 3)
         multiply(LAST, 3)
-        flip_cells(LAST, 1)
-        sum_up(LAST - 1, 2)
-        sum_up(LAST - 1, 3)
         weigh(LAST, 0)
+        sum_up(LAST - 1, 0)
+        sum_up(LAST, 0)
+        flip_cells(LAST, 1)
+        for ft in range(1, FEATURE_TILES):
+            sum_up(LAST - 1, ft)
         add_input_term(LAST, 2)
         squash(LAST, 2)
+        store_out(0)
         weigh(LAST, 1)
+        sum_up(LAST, 1)
         add_input_term(LAST, 3)
         squash(LAST, 3)
-        sum_up(LAST, 0)
-        sum_up(LAST, 1)
-        store_out(0)
         store_out(1)
         weigh(LAST, 2)
         sum_up(LAST, 2)

@@ -41,7 +41,7 @@ GROUPED_BUFS = 4
 SUM_LAG = 4
 SUM_EARLY = True
 HEAD_SHARES = (224, 0)
-SHARES = ((0, 192), (96, 80), (96, 80), (0, 192), (0, 192))
+SHARES = ((0, 176), (128, 64), (128, 64), (0, 176), (0, 176))
 RUN = 8
 
 FLOPS = 2 * NODES * (CHILDREN * FEATURES) ** 2 + 2 * NODES * FEATURES * FEATURES
@@ -333,24 +333,27 @@ def tile_treelstmcell_pa_kernel(
             for g in passes:
                 one_pass(child, ft, g)
 
-        def add_input_term(child, ft):
-            pre = work.tile([P, NODES], F32, tag="pre")
+        def add_input_term(child, ft, nodes=slice(0, NODES)):
+            if nodes.start == 0:
+                pre_of[(child, ft)] = work.tile([P, NODES], F32, tag="pre", name="pre")
             nc.vector.tensor_tensor(
-                out=pre[:], in0=acc_of[(child, ft)][:], in1=input_term[ft][:], op=ADD
+                out=pre_of[(child, ft)][:, nodes],
+                in0=acc_of[(child, ft)][:, nodes],
+                in1=input_term[ft][:, nodes],
+                op=ADD,
             )
-            pre_of[(child, ft)] = pre
 
-        def squash(child, ft):
-            gate = work.tile([P, NODES], F32, tag="gate")
+        def squash(child, ft, nodes=slice(0, NODES)):
+            if nodes.start == 0:
+                gate_of[(child, ft)] = work.tile([P, NODES], F32, tag="gate", name="gate")
             tile_index = child * FEATURE_TILES + ft
             nc.scalar.activation(
-                out=gate[:],
-                in_=pre_of[(child, ft)][:],
+                out=gate_of[(child, ft)][:, nodes],
+                in_=pre_of[(child, ft)][:, nodes],
                 func=SIGMOID,
                 bias=bias_cols[:, tile_index : tile_index + 1],
                 scale=1.0,
             )
-            gate_of[(child, ft)] = gate
 
         def flip_cells(child, pair):
             bank = psum_flip.tile([P, 2, NODES], BF16, tag="flip")
@@ -364,19 +367,21 @@ def tile_treelstmcell_pa_kernel(
                     )
             cells_t[(child, pair)] = bank
 
-        def weigh(child, ft):
-            weighted = work.tile([P, NODES], F32, tag="weighted", bufs=8)
+        def weigh(child, ft, nodes=slice(0, NODES)):
+            if nodes.start == 0:
+                weighted_of[(child, ft)] = work.tile(
+                    [P, NODES], F32, tag="weighted", name="weighted", bufs=8
+                )
             nc.vector.tensor_tensor(
-                out=weighted[:],
-                in0=gate_of[(child, ft)][:],
-                in1=cells_t[(child, ft // 2)][:, ft % 2, :],
+                out=weighted_of[(child, ft)][:, nodes],
+                in0=gate_of[(child, ft)][:, nodes],
+                in1=cells_t[(child, ft // 2)][:, ft % 2, nodes],
                 op=MULT,
             )
-            weighted_of[(child, ft)] = weighted
 
-        def sum_up(child, ft):
+        def sum_up(child, ft, tiles=range(NODE_TILES)):
             weighted = weighted_of[(child, ft)]
-            for nt in range(NODE_TILES):
+            for nt in tiles:
                 nc.tensor.matmul(
                     out=out_sums[ft][:, nt, :],
                     lhsT=weighted[:, nt * P : (nt + 1) * P],
@@ -470,19 +475,23 @@ def tile_treelstmcell_pa_kernel(
         sum_up(LAST - 1, 0)
         sum_up(LAST, 0)
         flip_cells(LAST, 1)
-        for ft in range(1, FEATURE_TILES):
-            sum_up(LAST - 1, ft)
+        sum_up(LAST - 1, 1)
         add_input_term(LAST, 2)
         squash(LAST, 2)
         store_out(0)
         weigh(LAST, 1)
         sum_up(LAST, 1)
-        add_input_term(LAST, 3)
-        squash(LAST, 3)
+        sum_up(LAST - 1, 2)
+        sum_up(LAST - 1, 3)
+        halves = (slice(0, NODES),)
+        for nodes in halves:
+            add_input_term(LAST, 3, nodes)
+            squash(LAST, 3, nodes)
         store_out(1)
         weigh(LAST, 2)
         sum_up(LAST, 2)
         store_out(2)
-        weigh(LAST, 3)
-        sum_up(LAST, 3)
+        for half, nodes in enumerate(halves):
+            weigh(LAST, 3, nodes)
+            sum_up(LAST, 3)
         store_out(3)

@@ -140,8 +140,8 @@ def tile_treelstmcell_pa_kernel(
             scalar_from = gpsimd_cols + vector_cols
             if gpsimd_cols:
                 nc.gpsimd.tensor_scalar(
-                    out=grouped[:, :gpsimd_cols, :],
-                    in0=raw[:, :, :gpsimd_cols].rearrange("p t c -> p c t"),
+                    out=grouped[:, :gpsimd_cols, :].rearrange("p (c i) t -> p c t i", i=RUN),
+                    in0=raw[:, :, :gpsimd_cols].rearrange("p t (c i) -> p c t i", i=RUN),
                     scalar1=1.0,
                     scalar2=0.0,
                     op0=MULT,

@@ -27,7 +27,7 @@ AGGR_TILES = CHILDREN * FEATURE_TILES
 
 RAW_BUFS = 10
 GPSIMD_COLS = 224
-CELLS_BEHIND = 1
+CELLS_BEHIND = 2
 S_OUT = (0, 1, 2)
 GATE = True
 GATE_FROM = 5
@@ -41,7 +41,7 @@ GROUPED_BUFS = 4
 SUM_LAG = 4
 SUM_EARLY = True
 HEAD_SHARES = (224, 0)
-SHARES = ((0, 176), (128, 64), (128, 64), (0, 176), (0, 176))
+SHARES = ((0, 192), (128, 64), (128, 64), (0, 192), (0, 192))
 RUN = 8
 
 FLOPS = 2 * NODES * (CHILDREN * FEATURES) ** 2 + 2 * NODES * FEATURES * FEATURES

from contextlib import ExitStack

import concourse.mybir as mybir
from concourse.masks import make_identity

F32 = mybir.dt.float32
BF16 = mybir.dt.bfloat16
U32 = mybir.dt.uint32
U8 = mybir.dt.uint8
FP8X4 = mybir.dt.float8_e4m3fn_x4
ADD = mybir.AluOpType.add
MULT = mybir.AluOpType.mult
SIGMOID = mybir.ActivationFunctionType.Sigmoid

P = 128
PACK = 4
K_PASS = P * PACK
NODES = 512
CHILDREN = 5
FEATURES = 512
NODE_TILES = NODES // P
FEATURE_TILES = FEATURES // P
H_PASSES = CHILDREN * FEATURES // K_PASS
CHUNKS = CHILDREN * H_PASSES
HALF = NODES // 2
AGGR_TILES = CHILDREN * FEATURE_TILES

RAW_BUFS = 10
GPSIMD_COLS = 224
CELLS_BEHIND = 2
S_OUT = (0, 1, 2)
GATE = True
GATE_FROM = 5
STT_AT = 5
HEAD_SLOTS = 5
VE = 5
W_AT = 4
FI_AT = 3
FLIPPED_BUFS = 6
GROUPED_BUFS = 4
SUM_LAG = 4
SUM_EARLY = True
HEAD_SHARES = (224, 0)
SHARES = ((0, 192), (128, 64), (128, 64), (0, 192), (0, 192))
RUN = 8

FLOPS = 2 * NODES * (CHILDREN * FEATURES) ** 2 + 2 * NODES * FEATURES * FEATURES


def tile_treelstmcell_pa_kernel(
    tc, x, x_mask, neighbour_h, neighbour_c, W_f_in, b_f_in, W_aggr_f, b_aggr_f, out
):
    nc = tc.nc
    hf = neighbour_h.rearrange("n c f -> n (c f)")

    with ExitStack() as stack:
        const = stack.enter_context(tc.tile_pool(name="const", bufs=1))
        raw_pool = stack.enter_context(tc.tile_pool(name="raw", bufs=RAW_BUFS))
        stage = stack.enter_context(tc.tile_pool(name="stage", bufs=3))
        codes_pool = stack.enter_context(tc.tile_pool(name="codes", bufs=2))
        work = stack.enter_context(tc.tile_pool(name="work", bufs=5))
        psum_out = stack.enter_context(tc.psum_pool(name="psum_out", bufs=1))
        psum_acc = stack.enter_context(tc.psum_pool(name="psum_acc", bufs=2))
        psum_flip = stack.enter_context(tc.psum_pool(name="psum_flip", bufs=2))
        stack.enter_context(tc.manual_schedule())

        warm = const.tile([P, 2], F32)
        nc.vector.memset(warm[:], 0.0)
        nc.scalar.activation(out=warm[:, 1:2], in_=warm[:, 0:1], func=SIGMOID)

        x_sb = const.tile([P, NODE_TILES * FEATURES], BF16)
        nc.sync.dma_start(
            out=x_sb[:].rearrange("p (t k) -> p t k", t=NODE_TILES),
            in_=x.rearrange("(t p) k -> p t k", p=P),
        )
        wf_raw = const.tile([P, PACK, FEATURES], BF16)
        nc.sync.dma_start(out=wf_raw[:], in_=W_f_in.rearrange("(p t) n -> p t n", t=PACK))

        bias_rows = const.tile([P, P], BF16)
        nc.vector.memset(bias_rows[:], 0.0)
        nc.sync.dma_start(
            out=bias_rows[0:AGGR_TILES, :], in_=b_aggr_f.rearrange("(r m) -> r m", m=P)
        )
        nc.sync.dma_start(
            out=bias_rows[AGGR_TILES : AGGR_TILES + FEATURE_TILES, :],
            in_=b_f_in.rearrange("(r m) -> r m", m=P),
        )
        mask_rows = const.tile([P, NODES], BF16)
        nc.vector.memset(mask_rows[:], 0.0)
        nc.sync.dma_start(out=mask_rows[0:1, :], in_=x_mask.rearrange("(o n) -> o n", o=1))

        h_sb = []
        raw_of = {}
        c_sb = {}

        def load_nodes(nt):
            h_tile = const.tile([P, CHILDREN * FEATURES], BF16, name="h_sb%d" % nt)
            nc.sync.dma_start(out=h_tile[:], in_=hf[nt * P : (nt + 1) * P, :])
            h_sb.append(h_tile)

        def load_cells(child):
            cells = const.tile([P, NODE_TILES, FEATURES], BF16, name="c_sb%d" % child)
            nc.sync.dma_start(
                out=cells[:], in_=neighbour_c[:, child, :].rearrange("(t p) f -> p t f", p=P)
            )
            c_sb[child] = cells

        def load_chunk(chunk):
            child, g = divmod(chunk, H_PASSES)
            raw = raw_pool.tile([P, PACK, FEATURES], BF16, tag="raw")
            nc.sync.dma_start(
                out=raw[:],
                in_=W_aggr_f[
                    g * K_PASS : (g + 1) * K_PASS, child * FEATURES : (child + 1) * FEATURES
                ].rearrange("(p t) n -> p t n", t=PACK),
            )
            raw_of[chunk] = raw
            if g == CELLS_BEHIND and child > 0:
                load_cells(child - 1)

        for nt in range(NODE_TILES):
            if nt >= W_AT:
                load_chunk(nt - W_AT)
            load_nodes(nt)
        for chunk in range(NODE_TILES - W_AT, RAW_BUFS):
            load_chunk(chunk)

        ident_f32 = const.tile([P, P], F32)
        make_identity(nc, ident_f32[:])
        ident_bf = const.tile([P, P], BF16)
        make_identity(nc, ident_bf[:])
        twos = const.tile([P, P], BF16)
        nc.vector.memset(twos[:], 2.0)

        def quantise(grouped, codes, scales):
            nc.vector.quantize_mx(out=codes.bitcast(FP8X4), scales=scales, in_=grouped)

        def regroup_gs(raw, vector_cols, gpsimd_cols):
            grouped = stage.tile([P, FEATURES, PACK], BF16, tag="grouped", bufs=GROUPED_BUFS, align_bytes=64)
            scalar_from = gpsimd_cols + vector_cols
            if gpsimd_cols:
                nc.gpsimd.tensor_scalar(
                    out=grouped[:, :gpsimd_cols, :].rearrange("p (c i) t -> p c t i", i=RUN),
                    in0=raw[:, :, :gpsimd_cols].rearrange("p t (c i) -> p c t i", i=RUN),
                    scalar1=1.0,
                    scalar2=0.0,
                    op0=MULT,
                    op1=ADD,
                )
            nc.scalar.copy(
                out=grouped[:, scalar_from:, :].rearrange("p (c i) t -> p c t i", i=RUN),
                in_=raw[:, :, scalar_from:].rearrange("p t (c i) -> p c t i", i=RUN),
            )
            return grouped

        def regroup_v(raw, grouped, vector_cols, gpsimd_cols):
            if vector_cols:
                cols = slice(gpsimd_cols, gpsimd_cols + vector_cols)
                nc.vector.tensor_copy(
                    out=grouped[:, cols, :].rearrange("p (c i) t -> p c t i", i=RUN),
                    in_=raw[:, :, cols].rearrange("p t (c i) -> p c t i", i=RUN),
                )

        x_codes = const.tile([P, NODES], U32, align_bytes=64)
        x_scales = const.tile([P, NODES], U8, align_bytes=64)
        h_codes = const.tile([P, H_PASSES, NODES], U32, align_bytes=64)
        h_scales = const.tile([P, H_PASSES, NODES], U8, align_bytes=64)
        wf_codes = const.tile([P, FEATURES], U32, align_bytes=64)
        wf_scales = const.tile([P, FEATURES], U8, align_bytes=64)

        out_sums = [
            psum_out.tile([P, NODE_TILES, P], F32, name="out_sums%d" % ft)
            for ft in range(FEATURE_TILES)
        ]
        flips = []

        def flip_blocks(blocks):
            step = len(flips)
            flips.append(step)
            bank = out_sums[step % FEATURE_TILES]
            for j, (rows, codes, scales) in enumerate(blocks):
                pairs = rows.rearrange("n (p u) -> n u p", u=2)
                for u in range(2):
                    nc.tensor.transpose(bank[:, 2 * j + u, :], pairs[:, u, :], ident_f32[:])
            grouped = stage.tile([P, 2, P * PACK], BF16, tag="flipped", bufs=FLIPPED_BUFS, align_bytes=64)
            used = len(blocks)
            words_out = (
                grouped[:, :used, :]
                .rearrange("p j m -> p (j m)")
                .bitcast(F32)
                .rearrange("p (j n u) -> p j n u", j=used, u=2)
            )
            words_in = bank[:, : 2 * used, :].rearrange("p (j u) n -> p j n u", u=2)
            if step % VE != VE - 1:
                nc.scalar.copy(out=words_out, in_=words_in)
            else:
                nc.vector.tensor_copy(out=words_out, in_=words_in)
            return [
                (grouped[:, j, :], codes, scales) for j, (rows, codes, scales) in enumerate(blocks)
            ]

        def x_block(nt):
            nodes = slice(nt * P, (nt + 1) * P)
            words = x_sb[:].bitcast(F32)[:, nt * K_PASS // 2 : (nt + 1) * K_PASS // 2]
            return words, x_codes[:, nodes], x_scales[:, nodes]

        def h_block(nt, g):
            nodes = slice(nt * P, (nt + 1) * P)
            words = h_sb[nt][:].bitcast(F32)[:, g * K_PASS // 2 : (g + 1) * K_PASS // 2]
            return words, h_codes[:, g, nodes], h_scales[:, g, nodes]

        to_quantise = []

        def flip_in_turn(blocks):
            for first in range(0, len(blocks), 2):
                flipped = flip_blocks(blocks[first : first + 2])
                quantise_flipped()
                to_quantise.extend(flipped)

        def quantise_flipped():
            for item in to_quantise:
                quantise(*item)
            to_quantise.clear()

        flip_in_turn([x_block(nt) for nt in range(NODE_TILES)])
        wf_grouped = regroup_gs(wf_raw, 0, 224)
        quantise_flipped()
        bias_ps = psum_flip.tile([P, P], BF16, tag="flip")
        nc.tensor.transpose(bias_ps[:], bias_rows[:], ident_bf[:])
        bias_cols = const.tile([P, P], F32)
        nc.vector.tensor_copy(out=bias_cols[:], in_=bias_ps[:])

        mask_ps = psum_acc.tile([P, NODES], F32, tag="acc")
        nc.tensor.matmul(out=mask_ps[:], lhsT=twos[:], rhs=mask_rows[:], start=True, stop=True)
        double_mask = const.tile([P, NODES], F32)
        nc.vector.tensor_copy(out=double_mask[:], in_=mask_ps[:])


        input_term = {}
        input_products = {}

        def multiply_input(ft):
            cols = slice(ft * P, (ft + 1) * P)
            product = out_sums[ft][:].rearrange("p t n -> p (t n)")
            nc.tensor.matmul_mx(
                out=product,
                lhsT=wf_codes[:, cols].bitcast(FP8X4),
                lhsT_scale=wf_scales[:, cols],
                rhs=x_codes[:].bitcast(FP8X4),
                rhs_scale=x_scales[:],
                start=True,
                stop=True,
            )
            input_products[ft] = product

        def finish_input_term(ft):
            term = const.tile([P, NODES], F32, name="input_term%d" % ft)
            nc.vector.scalar_tensor_tensor(
                out=term[:],
                in0=input_products[ft],
                scalar=bias_cols[:, AGGR_TILES + ft : AGGR_TILES + ft + 1],
                in1=double_mask[:],
                op0=ADD,
                op1=MULT,
            )
            input_term[ft] = term

        grouped_of = {}
        for nt in range(NODE_TILES):
            if nt >= W_AT:
                grouped_of[nt - W_AT] = regroup_gs(raw_of[nt - W_AT], *HEAD_SHARES)
                regroup_v(raw_of[nt - W_AT], grouped_of[nt - W_AT], *HEAD_SHARES)
            flip_in_turn([h_block(nt, g) for g in range(H_PASSES)])
            if nt == FI_AT:
                for ft in range(FEATURE_TILES):
                    multiply_input(ft)
            if nt == 0:
                quantise(wf_grouped[:].rearrange("p c t -> p (c t)"), wf_codes[:], wf_scales[:])
        quantise_flipped()


        w_codes = {}
        w_scales = {}
        acc_of = {}
        pre_of = {}
        gate_of = {}
        weighted_of = {}
        cells_t = {}

        gate_word = const.tile([P, 1], U32)

        def hold_gpsimd(chunk):
            child, g = divmod(chunk, H_PASSES)
            nc.gpsimd.tensor_copy(out=gate_word[:], in_=w_codes[child][:, g, 0:1])

        def quantise_chunk(chunk):
            child, g = divmod(chunk, H_PASSES)
            if g == 0:
                w_codes[child] = codes_pool.tile(
                    [P, H_PASSES, FEATURES], U32, tag="w_codes", name="w_codes", align_bytes=64
                )
                w_scales[child] = codes_pool.tile(
                    [P, H_PASSES, FEATURES], U8, tag="w_scales", name="w_scales", align_bytes=64
                )
            quantise(
                grouped_of[chunk][:].rearrange("p c t -> p (c t)"),
                w_codes[child][:, g, :],
                w_scales[child][:, g, :],
            )

        def one_pass(child, ft, g):
            cols = slice(ft * P, (ft + 1) * P)
            nc.tensor.matmul_mx(
                out=acc_of[(child, ft)][:],
                lhsT=w_codes[child][:, g, cols].bitcast(FP8X4),
                lhsT_scale=w_scales[child][:, g, cols],
                rhs=h_codes[:, g, :].bitcast(FP8X4),
                rhs_scale=h_scales[:, g, :],
                start=(g == 0),
                stop=(g == H_PASSES - 1),
            )

        def multiply_chunk(child, g):
            for ft in range(FEATURE_TILES):
                if g == 0:
                    pool, tag = (psum_flip, "flip") if ft < 2 else (psum_acc, "acc")
                    acc_of[(child, ft)] = pool.tile([P, NODES], F32, tag=tag, name="acc_first")
                one_pass(child, ft, g)

        def multiply(child, ft, passes=range(H_PASSES)):
            if 0 in passes:
                acc_of[(child, ft)] = psum_acc.tile([P, NODES], F32, tag="acc", name="acc")
            for g in passes:
                one_pass(child, ft, g)

        def add_input_term(child, ft, nodes=slice(0, NODES)):
            if nodes.start == 0:
                pre_of[(child, ft)] = work.tile([P, NODES], F32, tag="pre", name="pre")
            nc.vector.tensor_tensor(
                out=pre_of[(child, ft)][:, nodes],
                in0=acc_of[(child, ft)][:, nodes],
                in1=input_term[ft][:, nodes],
                op=ADD,
            )

        def squash(child, ft, nodes=slice(0, NODES)):
            if nodes.start == 0:
                gate_of[(child, ft)] = work.tile([P, NODES], F32, tag="gate", name="gate")
            tile_index = child * FEATURE_TILES + ft
            nc.scalar.activation(
                out=gate_of[(child, ft)][:, nodes],
                in_=pre_of[(child, ft)][:, nodes],
                func=SIGMOID,
                bias=bias_cols[:, tile_index : tile_index + 1],
                scale=1.0,
            )

        def flip_cells(child, pair):
            bank = psum_flip.tile([P, 2, NODES], BF16, tag="flip")
            for side in range(2):
                ft = 2 * pair + side
                for nt in range(NODE_TILES):
                    nc.tensor.transpose(
                        bank[:, side, nt * P : (nt + 1) * P],
                        c_sb[child][:, nt, ft * P : (ft + 1) * P],
                        ident_bf[:],
                    )
            cells_t[(child, pair)] = bank

        def weigh(child, ft, nodes=slice(0, NODES)):
            if nodes.start == 0:
                weighted_of[(child, ft)] = work.tile(
                    [P, NODES], F32, tag="weighted", name="weighted", bufs=8
                )
            nc.vector.tensor_tensor(
                out=weighted_of[(child, ft)][:, nodes],
                in0=gate_of[(child, ft)][:, nodes],
                in1=cells_t[(child, ft // 2)][:, ft % 2, nodes],
                op=MULT,
            )

        def sum_up(child, ft, tiles=range(NODE_TILES)):
            weighted = weighted_of[(child, ft)]
            for nt in tiles:
                nc.tensor.matmul(
                    out=out_sums[ft][:, nt, :],
                    lhsT=weighted[:, nt * P : (nt + 1) * P],
                    rhs=ident_f32[:],
                    is_transpose=True,
                    start=(child == 0 and nt == 0),
                    stop=(child == CHILDREN - 1 and nt == NODE_TILES - 1),
                )

        def store_out(ft):
            result = work.tile([P, NODE_TILES, P], F32, tag="result", bufs=4)
            if ft in S_OUT:
                nc.scalar.copy(out=result[:], in_=out_sums[ft][:])
            else:
                nc.vector.tensor_copy(out=result[:], in_=out_sums[ft][:])
            nc.sync.dma_start(
                out=out.rearrange("(t p) f -> p t f", p=P)[:, :, ft * P : (ft + 1) * P],
                in_=result[:],
            )

        def tile_at(slot, lag):
            child, ft = divmod(slot - H_PASSES - lag, H_PASSES)
            if 0 <= child < CHILDREN and ft < FEATURE_TILES:
                return child, ft
            return None

        LAST = CHILDREN - 1
        for slot in range(CHUNKS):
            child, place = divmod(slot - H_PASSES, H_PASSES)
            first, middle, leaving = [tile_at(slot, lag) for lag in (0, 2, 3)]
            if slot < CHUNKS:
                shares = HEAD_SHARES if slot < HEAD_SLOTS else SHARES[place]
                if GATE and slot >= GATE_FROM and shares[1]:
                    hold_gpsimd(slot - 2)
                grouped_of[slot] = regroup_gs(raw_of[slot], *shares)
            if STT_AT <= slot < STT_AT + 2:
                for ft in range(2):
                    finish_input_term(2 * (slot - STT_AT) + ft)
            if middle is not None:
                add_input_term(*middle)
            if slot == CHUNKS - 1:
                multiply(LAST, 0, range(3))
            if leaving is not None:
                weigh(*leaving)
            if place == 2:
                if child > 0:
                    sum_up(child - 1, 2)
                    sum_up(child - 1, 3)
                if child >= 0:
                    flip_cells(child, 0)
            if place == 4 and child >= 0:
                if slot < CHUNKS - 1:
                    sum_up(child, 0)
                    sum_up(child, 1)
                flip_cells(child, 1)
            if slot == CHUNKS - 1:
                add_input_term(LAST - 1, 3)
                multiply(LAST, 1, range(3))
            if first is not None and 0 < child < LAST:
                if place == 0:
                    multiply(child, 0, range(H_PASSES - 1))
                else:
                    if place == 1:
                        multiply(child, 0, [H_PASSES - 1])
                    multiply(child, place)
            if slot < CHUNKS:
                regroup_v(raw_of[slot], grouped_of[slot], *shares)
            if slot + RAW_BUFS < CHUNKS:
                load_chunk(slot + RAW_BUFS)
            if slot + RAW_BUFS == CHUNKS:
                load_cells(LAST)
            if slot >= 1:
                quantise_chunk(slot - 1)
                if slot <= H_PASSES:
                    multiply_chunk(0, slot - 1)
            if middle is not None:
                squash(*middle)
        squash(LAST - 1, 3)
        quantise_chunk(CHUNKS - 1)
        for ft in range(2):
            multiply(LAST, ft, range(3, H_PASSES))
        flip_cells(LAST, 0)
        for ft in range(2):
            add_input_term(LAST, ft)
            squash(LAST, ft)
        weigh(LAST - 1, 2)
        multiply(LAST, 2)
        weigh(LAST - 1, 3)
        multiply(LAST, 3)
        weigh(LAST, 0)
        sum_up(LAST - 1, 0)
        sum_up(LAST, 0)
        flip_cells(LAST, 1)
        sum_up(LAST - 1, 1)
        add_input_term(LAST, 2)
        squash(LAST, 2)
        store_out(0)
        weigh(LAST, 1)
        sum_up(LAST, 1)
        sum_up(LAST - 1, 2)
        sum_up(LAST - 1, 3)
        halves = (slice(0, NODES),)
        for nodes in halves:
            add_input_term(LAST, 3, nodes)
            squash(LAST, 3, nodes)
        store_out(1)
        weigh(LAST, 2)
        sum_up(LAST, 2)
        store_out(2)
        for half, nodes in enumerate(halves):
            weigh(LAST, 3, nodes)
            sum_up(LAST, 3)
        store_out(3)
